import numpy as np
import ml_dtypes


def mxq(x, axis, fmt="e4m3"):
    dtype, down = {"e4m3": (ml_dtypes.float8_e4m3fn, 7), "e5m2": (ml_dtypes.float8_e5m2, 14)}[fmt]
    v = np.moveaxis(np.asarray(x, np.float32).astype(ml_dtypes.bfloat16).astype(np.float64), axis, -1)
    blocks = v.reshape(v.shape[:-1] + (-1, 32))
    amax = np.abs(blocks).max(-1, keepdims=True)
    byte = np.maximum(np.where(amax > 0, np.frexp(amax)[1] - 1 + 127, 0) - down, 1)
    scale = np.exp2(byte - 127.0)
    codes = (blocks / scale).astype(np.float32).astype(dtype).astype(np.float64)
    return np.moveaxis((codes * scale).reshape(v.shape), -1, axis)


WIDE = False


def mx_kscale(k):
    if not WIDE:
        return np.ones(k)
    levels = np.array([10, -10, 5, -5, 0])
    a = np.random.permutation(np.resize(levels, k // 512 * 4)).reshape(k // 512, 4)
    idx = np.arange(k)
    return np.exp2(a[idx // 512, idx % 128 // 32])


BF16 = ml_dtypes.bfloat16


def bf(x):
    return np.asarray(x, np.float32).astype(BF16)


def f64(x):
    return np.asarray(x).astype(np.float64)


B, C, H, W = 4, 512, 64, 32
CH = C // 2
N = H * W
M = (H // 2) * (W // 2)
QS = 1.35 * CH ** -0.25


def pool2(t):
    r = t.reshape(B, -1, H // 2, 2, W // 2, 2)
    return r.max(axis=(3, 5)) + r.mean(axis=(3, 5))


def setup_inputs():
    s = mx_kscale(C)
    s = s / s.max()
    return {"x": bf(np.random.standard_normal((B, C, H, W)) * s[None, :, None, None]),
            "c2": bf(np.random.standard_normal((B, CH, H, W)) * QS),
            "c1p": bf((1.03 + 1.11 * np.random.standard_normal((B, CH, H // 2, W // 2))) * QS),
            "W3": bf(np.random.standard_normal((C, C)) / np.sqrt(C) / s),
            "gamma": bf(1.0 + 0.1 * np.random.standard_normal(1))}


def reference(x, c2, c1p, W3, gamma):
    c3 = mxq(f64(W3), 1, "e4m3") @ mxq(f64(x).reshape(B, C, N), 1, "e4m3")
    c3p = pool2(c3.reshape(B, C, H, W)).reshape(B, C, M)
    sc = f64(c2).reshape(B, CH, N).transpose(0, 2, 1) @ f64(c1p).reshape(B, CH, M)
    e = np.exp(sc - sc.max(-1, keepdims=True))
    num = mxq(c3p, 2, "e4m3") @ mxq(e.transpose(0, 2, 1), 1, "e4m3")
    refined = num / e.sum(-1)[:, None, :]
    return f64(gamma)[0] * refined.reshape(B, C, H, W) + f64(x)

@@ -1,0 +1,272 @@
+from contextlib import ExitStack
+
+import concourse.mybir as mybir
+from concourse.masks import make_identity
+
+F32 = mybir.dt.float32
+BF16 = mybir.dt.bfloat16
+U32 = mybir.dt.uint32
+U8 = mybir.dt.uint8
+FP8X4 = mybir.dt.float8_e4m3fn_x4
+ALU = mybir.AluOpType
+ACT = mybir.ActivationFunctionType
+AX = mybir.AxisListType
+
+B, C, H, W = 4, 512, 64, 32
+CH = C // 2
+N = H * W
+M = (H // 2) * (W // 2)
+P = 128
+FLOPS = 2 * B * (C * C * N + CH * N * M + C * M * N)
+
+NHALF = 2 * B
+TICKS = B * N // P
+LAG_TE = 3
+LAG_Q = 6
+LAG_RC = 5
+LAG_MX = 8
+PIN = True
+
+
+def tile_selfspatialattentionmodule_pb_t_kernel(tc, x, c2, c1p, W3, gamma, out):
+    nc = tc.nc
+    with ExitStack() as ctx:
+        if PIN:
+            ctx.enter_context(tc.manual_schedule())
+        keep = ctx.enter_context(tc.tile_pool(name="keep", bufs=1))
+        work = ctx.enter_context(tc.tile_pool(name="work", bufs=2))
+        psum = ctx.enter_context(tc.psum_pool(name="psum", bufs=1))
+
+        def bank(idx, shape, dtype, name):
+            return psum.tile(shape, dtype, name=name, tag="bank%d" % idx)
+
+        w3_sb = keep.tile([P, 4, C], BF16, name="w3_sb")
+        nc.sync.dma_start(out=w3_sb[:], in_=W3.rearrange("(p a) i -> p a i", a=4))
+        x_sb = []
+        for g in range(NHALF):
+            b, hf = divmod(g, 2)
+            cols = slice(hf * (N // 2), (hf + 1) * (N // 2))
+            x_sb.append(keep.tile([P, 4, N // 2], BF16, name="x_sb%d" % g))
+            nc.sync.dma_start(out=x_sb[g][:], in_=x[b].rearrange("(p j) h w -> p j (h w)", j=4)[:, :, cols])
+        c1_sb = []
+        c2_sb = []
+        for b in range(B):
+            c1_sb.append(keep.tile([P, 2, M], BF16, name="c1_sb%d" % b))
+            c2_sb.append(keep.tile([P, 2, N], BF16, name="c2_sb%d" % b))
+            nc.sync.dma_start(out=c1_sb[b][:], in_=c1p[b].rearrange("(g p) i j -> p g (i j)", g=2))
+            nc.sync.dma_start(out=c2_sb[b][:], in_=c2[b].rearrange("(g p) h w -> p g (h w)", g=2))
+        gam_bf = keep.tile([P, 1], BF16, name="gam_bf")
+        nc.sync.dma_start(out=gam_bf[:], in_=gamma.partition_broadcast(P))
+
+        ident_f = keep.tile([P, P], F32, name="ident_f")
+        make_identity(nc, ident_f[:])
+        ident_b = keep.tile([P, P], BF16, name="ident_b")
+        make_identity(nc, ident_b[:])
+        warm_in = keep.tile([P, 1], F32, name="warm_in")
+        warm_out = keep.tile([P, 1], F32, name="warm_out")
+        nc.vector.memset(warm_in[:], 0.0)
+        nc.scalar.activation(out=warm_out[:], in_=warm_in[:], func=ACT.Exp)
+
+        w3_words = w3_sb[:].bitcast(F32).rearrange("p a (q u) -> p a u q", u=2)
+        w3_g = keep.tile([P, C, 4], BF16, name="w3_g", align_bytes=64)
+        w3_g32 = w3_g[:].bitcast(F32)
+        for h in range(2):
+            w_t = bank(h, [P, 2, 2, P], F32, "w_t")
+            for u in range(2):
+                for a in range(2):
+                    nc.tensor.transpose(w_t[:, u, a, :], w3_words[:, 2 * h + a, u, :], ident_f[:])
+            nc.vector.tensor_copy(
+                out=w3_g32[:, 256 * h : 256 * h + 256, :].rearrange("p (a q) u -> p a q u", a=2),
+                in_=w_t[:].rearrange("p u a q -> p a q u"),
+            )
+        w3_q = keep.tile([P, C], U32, name="w3_q", align_bytes=64)
+        w3_s = keep.tile([P, C], U8, name="w3_s", align_bytes=64)
+
+        xg_t = {}
+        xq_t = {}
+        xs_t = {}
+
+        def regroup_x(g, engines):
+            xg = work.tile([P, 4, 256, 4], BF16, name="xg", tag="big", bufs=3, align_bytes=64)
+            xg_t[g] = xg
+            src = x_sb[g][:].rearrange(
+                "p j (i dh jj dw) -> p dh dw i jj j", i=16, dh=2, jj=16, dw=2
+            )
+            for mm in range(4):
+                dst = xg[:, mm, :, :].rearrange("p (i jj) j -> p i jj j", i=16)
+                s = src[:, mm // 2, mm % 2]
+                eng = engines[mm]
+                if eng == "v":
+                    nc.vector.tensor_copy(out=dst, in_=s)
+                elif eng == "s":
+                    nc.scalar.copy(out=dst, in_=s)
+                else:
+                    nc.gpsimd.tensor_scalar(out=dst, in0=s, scalar1=1.0, scalar2=0.0, op0=ALU.mult, op1=ALU.add)
+
+        def quantise_x(g):
+            xq = work.tile([P, 1024], U32, name="xq", align_bytes=64)
+            xs = work.tile([P, 1024], U8, name="xs", align_bytes=64)
+            xq_t[g] = xq
+            xs_t[g] = xs
+            nc.vector.quantize_mx(
+                out=xq[:].bitcast(FP8X4), scales=xs[:], in_=xg_t[g][:].rearrange("p m q j -> p (m q j)")
+            )
+
+        regroup_x(0, "vvsg")
+        nc.vector.quantize_mx(out=w3_q[:].bitcast(FP8X4), scales=w3_s[:], in_=w3_g[:].rearrange("p c t -> p (c t)"))
+        quantise_x(0)
+        regroup_x(1, "vssg")
+
+        ring = [0]
+        c3pb_t = {}
+        c3q = []
+        c3s = []
+        for b in range(B):
+            c3q.append(keep.tile([P, C], U32, name="c3q%d" % b, align_bytes=64))
+            c3s.append(keep.tile([P, C], U8, name="c3s%d" % b, align_bytes=64))
+        c3g_t = {}
+
+        def quantise_c3p(b):
+            nc.vector.quantize_mx(
+                out=c3q[b][:].bitcast(FP8X4), scales=c3s[b][:], in_=c3g_t[b][:].rearrange("p c t -> p (c t)")
+            )
+
+        def mx1(dst, g, mm, tl, start, stop):
+            cols = slice(mm * 256 + tl * P, mm * 256 + tl * P + P)
+            nc.tensor.matmul_mx(
+                out=dst[:],
+                lhsT=xq_t[g][:, cols].bitcast(FP8X4),
+                lhsT_scale=xs_t[g][:, cols],
+                rhs=w3_q[:].bitcast(FP8X4),
+                rhs_scale=w3_s[:],
+                start=start,
+                stop=stop,
+            )
+
+        for g in range(NHALF):
+            b, hf = divmod(g, 2)
+            if hf == 0:
+                c3pb_t[b] = work.tile([P, 4, C], BF16, name="c3pb", tag="mid", bufs=3)
+            c3 = {}
+            acc = {}
+            for mm in range(4):
+                for tl in range(2):
+                    c3[mm, tl] = bank(ring[0] % 6, [P, C], F32, "c3")
+                    ring[0] += 1
+                    mx1(c3[mm, tl], g, mm, tl, True, True)
+                    if mm == 0:
+                        acc[tl] = work.tile([P, C], F32, name="acc%d" % tl)
+                        nc.scalar.copy(out=acc[tl][:], in_=c3[mm, tl][:])
+                    else:
+                        nc.vector.tensor_tensor(out=acc[tl][:], in0=acc[tl][:], in1=c3[mm, tl][:], op=ALU.max)
+            if g + 1 < NHALF:
+                quantise_x(g + 1)
+            if hf == 0 and b > 0:
+                quantise_c3p(b - 1)
+            for tl in range(2):
+                tot = bank(6 + tl, [P, C], F32, "tot")
+                for mm in range(4):
+                    mx1(tot, g, mm, tl, mm == 0, mm == 3)
+                nc.vector.scalar_tensor_tensor(
+                    out=c3pb_t[b][:, 2 * hf + tl, :], in0=tot[:], scalar=0.25, in1=acc[tl][:], op0=ALU.mult, op1=ALU.add
+                )
+            if g + 2 < NHALF:
+                regroup_x(g + 2, "sssg")
+            if hf == 1:
+                c3g = work.tile([P, C, 4], BF16, name="c3g", tag="grp", bufs=2, align_bytes=64)
+                c3g_t[b] = c3g
+                nc.gpsimd.tensor_scalar(
+                    out=c3g[:], in0=c3pb_t[b][:].rearrange("p t c -> p c t"), scalar1=1.0, scalar2=0.0,
+                    op0=ALU.mult, op1=ALU.add,
+                )
+        quantise_c3p(B - 1)
+        gam = keep.tile([P, 1], F32, name="gam")
+        nc.vector.tensor_copy(out=gam[:], in_=gam_bf[:])
+
+        sc_t = {}
+        nmx_t = {}
+        sum_t = {}
+        e_t = {}
+        eg_t = {}
+        eq_t = {}
+        es_t = {}
+        rcp_t = {}
+        r_t = {}
+        y_t = {}
+        out_v = [out[b].rearrange("(p j) h w -> p j (h w)", j=4) for b in range(B)]
+
+        for t in range(TICKS + LAG_MX):
+            if t >= LAG_RC and (t - LAG_RC) % 4 == 0 and (t - LAG_RC) // 4 < TICKS // 4:
+                k = (t - LAG_RC) // 4
+                rcp_t[k] = work.tile([P, 4], F32, name="rcp", bufs=2)
+                nc.vector.reciprocal(out=rcp_t[k][:], in_=sum_t[k][:])
+            if t < TICKS:
+                k, i = divmod(t, 4)
+                b = k // 4
+                n0 = (k % 4) * 512 + i * P
+                if i == 0:
+                    nmx_t[k] = work.tile([P, 4], F32, name="nmx", bufs=3)
+                    sum_t[k] = work.tile([P, 4], F32, name="sums", bufs=3)
+                    e_t[k] = work.tile([P, 4, M], BF16, name="e_bf", tag="mid", bufs=3)
+                sc = bank(t % 3, [P, M], F32, "sc")
+                for h in range(2):
+                    nc.tensor.matmul(
+                        out=sc[:], lhsT=c2_sb[b][:, h, n0 : n0 + P], rhs=c1_sb[b][:, h, :], start=h == 0, stop=h == 1
+                    )
+                nc.vector.tensor_reduce(out=nmx_t[k][:, i : i + 1], in_=sc[:], axis=AX.X, op=ALU.max, negate=True)
+                nc.scalar.activation(
+                    out=e_t[k][:, i, :], in_=sc[:], func=ACT.Exp, bias=nmx_t[k][:, i : i + 1], scale=1.0,
+                    accum_out=sum_t[k][:, i : i + 1],
+                )
+            if t >= LAG_MX:
+                k, j = divmod(t - LAG_MX, 4)
+                b = k // 4
+                cols = slice((k % 4) * 512, (k % 4) * 512 + 512)
+                if j == 0:
+                    y_t[k] = work.tile([P, 4, 512], F32, name="y", tag="big", bufs=3, align_bytes=64)
+                num = bank(3 + t % 2, [P, 512], F32, "num")
+                nc.tensor.matmul_mx(
+                    out=num[:],
+                    lhsT=c3q[b][:, j * P : j * P + P].bitcast(FP8X4),
+                    lhsT_scale=c3s[b][:, j * P : j * P + P],
+                    rhs=eq_t[k][:].bitcast(FP8X4),
+                    rhs_scale=es_t[k][:],
+                    start=True,
+                    stop=True,
+                )
+                nc.vector.scalar_tensor_tensor(
+                    out=y_t[k][:, j, :], in0=num[:], scalar=gam[:, 0:1], in1=r_t[k][:], op0=ALU.mult, op1=ALU.mult
+                )
+                nc.gpsimd.tensor_tensor(out=y_t[k][:, j, :], in0=y_t[k][:, j, :], in1=x_sb[k // 2][:, j, (k % 2) * 512 : (k % 2) * 512 + 512], op=ALU.add)
+                if j == 3:
+                    nc.sync.dma_start(out=out_v[b][:, :, cols], in_=y_t[k][:])
+            if t >= LAG_Q and (t - LAG_Q) % 4 == 0 and (t - LAG_Q) // 4 < TICKS // 4:
+                k = (t - LAG_Q) // 4
+                eq_t[k] = work.tile([P, 512], U32, name="eq", align_bytes=64)
+                es_t[k] = work.tile([P, 512], U8, name="es", align_bytes=64)
+                nc.vector.quantize_mx(
+                    out=eq_t[k][:].bitcast(FP8X4), scales=es_t[k][:], in_=eg_t[k][:].rearrange("p n t -> p (n t)")
+                )
+            if t >= LAG_TE and (t - LAG_TE) % 2 == 0 and (t - LAG_TE) // 2 < TICKS // 2:
+                pr = (t - LAG_TE) // 2
+                k, half = divmod(pr, 2)
+                if half == 0:
+                    eg_t[k] = work.tile([P, 512, 4], BF16, name="eg", tag="grp", bufs=2, align_bytes=64)
+                e_tr = bank(5 + pr % 2, [P, 2, 4, P], BF16, "e_tr")
+                for i2 in range(2):
+                    for tt in range(4):
+                        nc.tensor.transpose(
+                            e_tr[:, i2, tt, :], e_t[k][:, 2 * half + i2, tt * P : tt * P + P], ident_b[:]
+                        )
+                nc.scalar.copy(
+                    out=eg_t[k][:, 256 * half : 256 * half + 256, :].rearrange("p (i n) t -> p i n t", i=2),
+                    in_=e_tr[:].rearrange("p i t n -> p i n t"),
+                )
+                if half == 1:
+                    r_ps = bank(7, [P, 512], F32, "r_ps")
+                    for i in range(4):
+                        nc.tensor.transpose(
+                            r_ps[:, i * P : i * P + P], rcp_t[k][:, i : i + 1].to_broadcast([P, P]), ident_f[:]
+                        )
+                    r_t[k] = work.tile([P, 512], F32, name="r_sb")
+                    nc.scalar.copy(out=r_t[k][:], in_=r_ps[:])

@@ -21,18 +21,25 @@ FLOPS = 2 * B * (C * C * N + CH * N * M + C * M * N)
 
 NHALF = 2 * B
 TICKS = B * N // P
+CHUNKS = TICKS // 4
 LAG_TE = 3
-LAG_Q = 6
 LAG_RC = 5
+LAG_Q = 6
 LAG_MX = 8
-PIN = True
+HEAD = 8
+RG0 = "vvgg"
+RG1 = "vsgg"
+RGN = "sssg"
+TAIL_V = 8
+X_AT = {4: 0, 7: 1}
+QX_AT = 8
+W3_AT = 2
 
 
 def tile_selfspatialattentionmodule_pb_t_kernel(tc, x, c2, c1p, W3, gamma, out):
     nc = tc.nc
     with ExitStack() as ctx:
-        if PIN:
-            ctx.enter_context(tc.manual_schedule())
+        ctx.enter_context(tc.manual_schedule())
         keep = ctx.enter_context(tc.tile_pool(name="keep", bufs=1))
         work = ctx.enter_context(tc.tile_pool(name="work", bufs=2))
         psum = ctx.enter_context(tc.psum_pool(name="psum", bufs=1))
@@ -40,47 +47,65 @@ def tile_selfspatialattentionmodule_pb_t_kernel(tc, x, c2, c1p, W3, gamma, out):
         def bank(idx, shape, dtype, name):
             return psum.tile(shape, dtype, name=name, tag="bank%d" % idx)
 
+        x_sb = [keep.tile([P, 4, N // 2], BF16, name="x_sb%d" % g) for g in range(NHALF)]
+        c2_sb = [keep.tile([P, 2, N // 2], BF16, name="c2_sb%d" % g) for g in range(NHALF)]
+        c1_sb = [keep.tile([P, 2, M], BF16, name="c1_sb%d" % b) for b in range(B)]
         w3_sb = keep.tile([P, 4, C], BF16, name="w3_sb")
-        nc.sync.dma_start(out=w3_sb[:], in_=W3.rearrange("(p a) i -> p a i", a=4))
-        x_sb = []
-        for g in range(NHALF):
-            b, hf = divmod(g, 2)
-            cols = slice(hf * (N // 2), (hf + 1) * (N // 2))
-            x_sb.append(keep.tile([P, 4, N // 2], BF16, name="x_sb%d" % g))
-            nc.sync.dma_start(out=x_sb[g][:], in_=x[b].rearrange("(p j) h w -> p j (h w)", j=4)[:, :, cols])
-        c1_sb = []
-        c2_sb = []
-        for b in range(B):
-            c1_sb.append(keep.tile([P, 2, M], BF16, name="c1_sb%d" % b))
-            c2_sb.append(keep.tile([P, 2, N], BF16, name="c2_sb%d" % b))
-            nc.sync.dma_start(out=c1_sb[b][:], in_=c1p[b].rearrange("(g p) i j -> p g (i j)", g=2))
-            nc.sync.dma_start(out=c2_sb[b][:], in_=c2[b].rearrange("(g p) h w -> p g (h w)", g=2))
         gam_bf = keep.tile([P, 1], BF16, name="gam_bf")
-        nc.sync.dma_start(out=gam_bf[:], in_=gamma.partition_broadcast(P))
 
-        ident_f = keep.tile([P, P], F32, name="ident_f")
-        make_identity(nc, ident_f[:])
+        def load_x(g):
+            cols = slice((g % 2) * (N // 2), (g % 2 + 1) * (N // 2))
+            nc.sync.dma_start(out=x_sb[g][:], in_=x[g // 2].rearrange("(p j) h w -> p j (h w)", j=4)[:, :, cols])
+
+        def load_c2(g):
+            cols = slice((g % 2) * (N // 2), (g % 2 + 1) * (N // 2))
+            nc.sync.dma_start(out=c2_sb[g][:], in_=c2[g // 2].rearrange("(g p) h w -> p g (h w)", g=2)[:, :, cols])
+
+        def load_c1(b):
+            nc.sync.dma_start(out=c1_sb[b][:], in_=c1p[b].rearrange("(g p) i j -> p g (i j)", g=2))
+
+        load_c1(0)
+        load_c2(0)
+        nc.sync.dma_start(out=w3_sb[:], in_=W3.rearrange("(p a) i -> p a i", a=4))
+        for g in range(NHALF):
+            load_x(g)
+        nc.sync.dma_start(out=gam_bf[:], in_=gamma.partition_broadcast(P))
+        load_c2(1)
+        for b in range(1, B):
+            load_c1(b)
+            load_c2(2 * b)
+            load_c2(2 * b + 1)
+
         ident_b = keep.tile([P, P], BF16, name="ident_b")
         make_identity(nc, ident_b[:])
+        ident_f = keep.tile([P, P], F32, name="ident_f")
+        make_identity(nc, ident_f[:])
         warm_in = keep.tile([P, 1], F32, name="warm_in")
         warm_out = keep.tile([P, 1], F32, name="warm_out")
         nc.vector.memset(warm_in[:], 0.0)
         nc.scalar.activation(out=warm_out[:], in_=warm_in[:], func=ACT.Exp)
 
-        w3_words = w3_sb[:].bitcast(F32).rearrange("p a (q u) -> p a u q", u=2)
         w3_g = keep.tile([P, C, 4], BF16, name="w3_g", align_bytes=64)
-        w3_g32 = w3_g[:].bitcast(F32)
-        for h in range(2):
-            w_t = bank(h, [P, 2, 2, P], F32, "w_t")
-            for u in range(2):
-                for a in range(2):
-                    nc.tensor.transpose(w_t[:, u, a, :], w3_words[:, 2 * h + a, u, :], ident_f[:])
-            nc.vector.tensor_copy(
-                out=w3_g32[:, 256 * h : 256 * h + 256, :].rearrange("p (a q) u -> p a q u", a=2),
-                in_=w_t[:].rearrange("p u a q -> p a q u"),
-            )
         w3_q = keep.tile([P, C], U32, name="w3_q", align_bytes=64)
         w3_s = keep.tile([P, C], U8, name="w3_s", align_bytes=64)
+
+        def prepare_w3():
+            w3_words = w3_sb[:].bitcast(F32).rearrange("p a (q u) -> p a u q", u=2)
+            w3_g32 = w3_g[:].bitcast(F32)
+            for h in range(2):
+                w_t = bank(3 + h, [P, 2, 2, P], F32, "w_t")
+                for u in range(2):
+                    for a in range(2):
+                        nc.tensor.transpose(w_t[:, u, a, :], w3_words[:, 2 * h + a, u, :], ident_f[:])
+                nc.vector.tensor_copy(
+                    out=w3_g32[:, 256 * h : 256 * h + 256, :].rearrange("p (a q) u -> p a q u", a=2),
+                    in_=w_t[:].rearrange("p u a q -> p a q u"),
+                )
+
+        def quantise_w3():
+            nc.vector.quantize_mx(
+                out=w3_q[:].bitcast(FP8X4), scales=w3_s[:], in_=w3_g[:].rearrange("p c t -> p (c t)")
+            )
 
         xg_t = {}
         xq_t = {}
@@ -89,13 +114,12 @@ def tile_selfspatialattentionmodule_pb_t_kernel(tc, x, c2, c1p, W3, gamma, out):
         def regroup_x(g, engines):
             xg = work.tile([P, 4, 256, 4], BF16, name="xg", tag="big", bufs=3, align_bytes=64)
             xg_t[g] = xg
-            src = x_sb[g][:].rearrange(
-                "p j (i dh jj dw) -> p dh dw i jj j", i=16, dh=2, jj=16, dw=2
-            )
-            for mm in range(4):
-                dst = xg[:, mm, :, :].rearrange("p (i jj) j -> p i jj j", i=16)
-                s = src[:, mm // 2, mm % 2]
-                eng = engines[mm]
+            src = x_sb[g][:].rearrange("p j (i dh jj dw) -> p dh i jj dw j", i=16, dh=2, jj=16, dw=2)
+            for piece in range(4):
+                dh, ih = divmod(piece, 2)
+                dst = xg[:, 2 * dh : 2 * dh + 2, P * ih : P * ih + P, :].rearrange("p dw (i jj) j -> p i jj dw j", i=8)
+                s = src[:, dh, 8 * ih : 8 * ih + 8]
+                eng = engines[piece]
                 if eng == "v":
                     nc.vector.tensor_copy(out=dst, in_=s)
                 elif eng == "s":
@@ -104,27 +128,17 @@ def tile_selfspatialattentionmodule_pb_t_kernel(tc, x, c2, c1p, W3, gamma, out):
                     nc.gpsimd.tensor_scalar(out=dst, in0=s, scalar1=1.0, scalar2=0.0, op0=ALU.mult, op1=ALU.add)
 
         def quantise_x(g):
-            xq = work.tile([P, 1024], U32, name="xq", align_bytes=64)
-            xs = work.tile([P, 1024], U8, name="xs", align_bytes=64)
-            xq_t[g] = xq
-            xs_t[g] = xs
+            xq_t[g] = work.tile([P, 1024], U32, name="xq", align_bytes=64)
+            xs_t[g] = work.tile([P, 1024], U8, name="xs", align_bytes=64)
             nc.vector.quantize_mx(
-                out=xq[:].bitcast(FP8X4), scales=xs[:], in_=xg_t[g][:].rearrange("p m q j -> p (m q j)")
+                out=xq_t[g][:].bitcast(FP8X4), scales=xs_t[g][:], in_=xg_t[g][:].rearrange("p m q j -> p (m q j)")
             )
 
-        regroup_x(0, "vvsg")
-        nc.vector.quantize_mx(out=w3_q[:].bitcast(FP8X4), scales=w3_s[:], in_=w3_g[:].rearrange("p c t -> p (c t)"))
-        quantise_x(0)
-        regroup_x(1, "vssg")
-
-        ring = [0]
+        c3q = [keep.tile([P, C], U32, name="c3q%d" % b, align_bytes=64) for b in range(B)]
+        c3s = [keep.tile([P, C], U8, name="c3s%d" % b, align_bytes=64) for b in range(B)]
         c3pb_t = {}
-        c3q = []
-        c3s = []
-        for b in range(B):
-            c3q.append(keep.tile([P, C], U32, name="c3q%d" % b, align_bytes=64))
-            c3s.append(keep.tile([P, C], U8, name="c3s%d" % b, align_bytes=64))
         c3g_t = {}
+        ring = [0]
 
         def quantise_c3p(b):
             nc.vector.quantize_mx(
@@ -143,22 +157,21 @@ def tile_selfspatialattentionmodule_pb_t_kernel(tc, x, c2, c1p, W3, gamma, out):
                 stop=stop,
             )
 
-        for g in range(NHALF):
+        def pool_half(g):
             b, hf = divmod(g, 2)
             if hf == 0:
                 c3pb_t[b] = work.tile([P, 4, C], BF16, name="c3pb", tag="mid", bufs=3)
-            c3 = {}
             acc = {}
             for mm in range(4):
                 for tl in range(2):
-                    c3[mm, tl] = bank(ring[0] % 6, [P, C], F32, "c3")
+                    c3 = bank(ring[0] % 6, [P, C], F32, "c3")
                     ring[0] += 1
-                    mx1(c3[mm, tl], g, mm, tl, True, True)
+                    mx1(c3, g, mm, tl, True, True)
                     if mm == 0:
                         acc[tl] = work.tile([P, C], F32, name="acc%d" % tl)
-                        nc.scalar.copy(out=acc[tl][:], in_=c3[mm, tl][:])
+                        nc.scalar.copy(out=acc[tl][:], in_=c3[:])
                     else:
-                        nc.vector.tensor_tensor(out=acc[tl][:], in0=acc[tl][:], in1=c3[mm, tl][:], op=ALU.max)
+                        nc.vector.tensor_tensor(out=acc[tl][:], in0=acc[tl][:], in1=c3[:], op=ALU.max)
             if g + 1 < NHALF:
                 quantise_x(g + 1)
             if hf == 0 and b > 0:
@@ -171,19 +184,14 @@ def tile_selfspatialattentionmodule_pb_t_kernel(tc, x, c2, c1p, W3, gamma, out):
                     out=c3pb_t[b][:, 2 * hf + tl, :], in0=tot[:], scalar=0.25, in1=acc[tl][:], op0=ALU.mult, op1=ALU.add
                 )
             if g + 2 < NHALF:
-                regroup_x(g + 2, "sssg")
+                regroup_x(g + 2, RGN)
             if hf == 1:
-                c3g = work.tile([P, C, 4], BF16, name="c3g", tag="grp", bufs=2, align_bytes=64)
-                c3g_t[b] = c3g
+                c3g_t[b] = work.tile([P, C, 4], BF16, name="c3g", tag="grp", bufs=2, align_bytes=64)
                 nc.gpsimd.tensor_scalar(
-                    out=c3g[:], in0=c3pb_t[b][:].rearrange("p t c -> p c t"), scalar1=1.0, scalar2=0.0,
+                    out=c3g_t[b][:], in0=c3pb_t[b][:].rearrange("p t c -> p c t"), scalar1=1.0, scalar2=0.0,
                     op0=ALU.mult, op1=ALU.add,
                 )
-        quantise_c3p(B - 1)
-        gam = keep.tile([P, 1], F32, name="gam")
-        nc.vector.tensor_copy(out=gam[:], in_=gam_bf[:])
 
-        sc_t = {}
         nmx_t = {}
         sum_t = {}
         e_t = {}
@@ -193,80 +201,127 @@ def tile_selfspatialattentionmodule_pb_t_kernel(tc, x, c2, c1p, W3, gamma, out):
         rcp_t = {}
         r_t = {}
         y_t = {}
+        gam = keep.tile([P, 1], F32, name="gam")
         out_v = [out[b].rearrange("(p j) h w -> p j (h w)", j=4) for b in range(B)]
 
-        for t in range(TICKS + LAG_MX):
-            if t >= LAG_RC and (t - LAG_RC) % 4 == 0 and (t - LAG_RC) // 4 < TICKS // 4:
-                k = (t - LAG_RC) // 4
-                rcp_t[k] = work.tile([P, 4], F32, name="rcp", bufs=2)
-                nc.vector.reciprocal(out=rcp_t[k][:], in_=sum_t[k][:])
-            if t < TICKS:
-                k, i = divmod(t, 4)
-                b = k // 4
-                n0 = (k % 4) * 512 + i * P
-                if i == 0:
-                    nmx_t[k] = work.tile([P, 4], F32, name="nmx", bufs=3)
-                    sum_t[k] = work.tile([P, 4], F32, name="sums", bufs=3)
-                    e_t[k] = work.tile([P, 4, M], BF16, name="e_bf", tag="mid", bufs=3)
-                sc = bank(t % 3, [P, M], F32, "sc")
-                for h in range(2):
-                    nc.tensor.matmul(
-                        out=sc[:], lhsT=c2_sb[b][:, h, n0 : n0 + P], rhs=c1_sb[b][:, h, :], start=h == 0, stop=h == 1
+        def front(t):
+            k, i = divmod(t, 4)
+            n0 = (k % 2) * 512 + i * P
+            if i == 0:
+                nmx_t[k] = work.tile([P, 4], F32, name="nmx", bufs=3)
+                sum_t[k] = work.tile([P, 4], F32, name="sums", bufs=3)
+                e_t[k] = work.tile([P, 4, M], BF16, name="e_bf", tag="mid", bufs=3)
+            sc = bank(t % 3, [P, M], F32, "sc")
+            for h in range(2):
+                nc.tensor.matmul(
+                    out=sc[:], lhsT=c2_sb[k // 2][:, h, n0 : n0 + P], rhs=c1_sb[k // 4][:, h, :], start=h == 0, stop=h == 1
+                )
+            nc.vector.tensor_reduce(out=nmx_t[k][:, i : i + 1], in_=sc[:], axis=AX.X, op=ALU.max, negate=True)
+            nc.scalar.activation(
+                out=e_t[k][:, i, :], in_=sc[:], func=ACT.Exp, bias=nmx_t[k][:, i : i + 1], scale=1.0,
+                accum_out=sum_t[k][:, i : i + 1],
+            )
+
+        def recip(k):
+            rcp_t[k] = work.tile([P, 4], F32, name="rcp", bufs=2)
+            nc.vector.reciprocal(out=rcp_t[k][:], in_=sum_t[k][:])
+
+        def quantise_e(k):
+            eq_t[k] = work.tile([P, 512], U32, name="eq", bufs=3, align_bytes=64)
+            es_t[k] = work.tile([P, 512], U8, name="es", bufs=3, align_bytes=64)
+            nc.vector.quantize_mx(
+                out=eq_t[k][:].bitcast(FP8X4), scales=es_t[k][:], in_=eg_t[k][:].rearrange("p n t -> p (n t)")
+            )
+
+        def turn(pr):
+            k, half = divmod(pr, 2)
+            if half == 0:
+                eg_t[k] = work.tile([P, 512, 4], BF16, name="eg", tag="grp", bufs=2, align_bytes=64)
+            e_tr = bank(5 + pr % 2, [P, 2, 4, P], BF16, "e_tr")
+            for i2 in range(2):
+                for tt in range(4):
+                    nc.tensor.transpose(e_tr[:, i2, tt, :], e_t[k][:, 2 * half + i2, tt * P : tt * P + P], ident_b[:])
+            nc.scalar.copy(
+                out=eg_t[k][:, 256 * half : 256 * half + 256, :].rearrange("p (i n) t -> p i n t", i=2),
+                in_=e_tr[:].rearrange("p i t n -> p i n t"),
+            )
+            if half == 1:
+                r_ps = bank(7, [P, 512], F32, "r_ps")
+                for i in range(4):
+                    nc.tensor.transpose(
+                        r_ps[:, i * P : i * P + P], rcp_t[k][:, i : i + 1].to_broadcast([P, P]), ident_f[:]
                     )
-                nc.vector.tensor_reduce(out=nmx_t[k][:, i : i + 1], in_=sc[:], axis=AX.X, op=ALU.max, negate=True)
-                nc.scalar.activation(
-                    out=e_t[k][:, i, :], in_=sc[:], func=ACT.Exp, bias=nmx_t[k][:, i : i + 1], scale=1.0,
-                    accum_out=sum_t[k][:, i : i + 1],
-                )
-            if t >= LAG_MX:
-                k, j = divmod(t - LAG_MX, 4)
-                b = k // 4
-                cols = slice((k % 4) * 512, (k % 4) * 512 + 512)
-                if j == 0:
-                    y_t[k] = work.tile([P, 4, 512], F32, name="y", tag="big", bufs=3, align_bytes=64)
-                num = bank(3 + t % 2, [P, 512], F32, "num")
-                nc.tensor.matmul_mx(
-                    out=num[:],
-                    lhsT=c3q[b][:, j * P : j * P + P].bitcast(FP8X4),
-                    lhsT_scale=c3s[b][:, j * P : j * P + P],
-                    rhs=eq_t[k][:].bitcast(FP8X4),
-                    rhs_scale=es_t[k][:],
-                    start=True,
-                    stop=True,
-                )
-                nc.vector.scalar_tensor_tensor(
-                    out=y_t[k][:, j, :], in0=num[:], scalar=gam[:, 0:1], in1=r_t[k][:], op0=ALU.mult, op1=ALU.mult
-                )
-                nc.gpsimd.tensor_tensor(out=y_t[k][:, j, :], in0=y_t[k][:, j, :], in1=x_sb[k // 2][:, j, (k % 2) * 512 : (k % 2) * 512 + 512], op=ALU.add)
-                if j == 3:
-                    nc.sync.dma_start(out=out_v[b][:, :, cols], in_=y_t[k][:])
-            if t >= LAG_Q and (t - LAG_Q) % 4 == 0 and (t - LAG_Q) // 4 < TICKS // 4:
-                k = (t - LAG_Q) // 4
-                eq_t[k] = work.tile([P, 512], U32, name="eq", align_bytes=64)
-                es_t[k] = work.tile([P, 512], U8, name="es", align_bytes=64)
-                nc.vector.quantize_mx(
-                    out=eq_t[k][:].bitcast(FP8X4), scales=es_t[k][:], in_=eg_t[k][:].rearrange("p n t -> p (n t)")
-                )
-            if t >= LAG_TE and (t - LAG_TE) % 2 == 0 and (t - LAG_TE) // 2 < TICKS // 2:
-                pr = (t - LAG_TE) // 2
-                k, half = divmod(pr, 2)
-                if half == 0:
-                    eg_t[k] = work.tile([P, 512, 4], BF16, name="eg", tag="grp", bufs=2, align_bytes=64)
-                e_tr = bank(5 + pr % 2, [P, 2, 4, P], BF16, "e_tr")
-                for i2 in range(2):
-                    for tt in range(4):
-                        nc.tensor.transpose(
-                            e_tr[:, i2, tt, :], e_t[k][:, 2 * half + i2, tt * P : tt * P + P], ident_b[:]
-                        )
-                nc.scalar.copy(
-                    out=eg_t[k][:, 256 * half : 256 * half + 256, :].rearrange("p (i n) t -> p i n t", i=2),
-                    in_=e_tr[:].rearrange("p i t n -> p i n t"),
-                )
-                if half == 1:
-                    r_ps = bank(7, [P, 512], F32, "r_ps")
-                    for i in range(4):
-                        nc.tensor.transpose(
-                            r_ps[:, i * P : i * P + P], rcp_t[k][:, i : i + 1].to_broadcast([P, P]), ident_f[:]
-                        )
-                    r_t[k] = work.tile([P, 512], F32, name="r_sb")
-                    nc.scalar.copy(out=r_t[k][:], in_=r_ps[:])
+                r_t[k] = work.tile([P, 512], F32, name="r_sb", bufs=3)
+                nc.scalar.copy(out=r_t[k][:], in_=r_ps[:])
+
+        def back(u):
+            k, j = divmod(u, 4)
+            b = k // 4
+            cols = slice((k % 4) * 512, (k % 4) * 512 + 512)
+            if j == 0:
+                y_t[k] = work.tile([P, 4, 512], F32, name="y", tag="big", bufs=3, align_bytes=64)
+            num = bank(3 + u % 2, [P, 512], F32, "num")
+            nc.tensor.matmul_mx(
+                out=num[:],
+                lhsT=c3q[b][:, j * P : j * P + P].bitcast(FP8X4),
+                lhsT_scale=c3s[b][:, j * P : j * P + P],
+                rhs=eq_t[k][:].bitcast(FP8X4),
+                rhs_scale=es_t[k][:],
+                start=True,
+                stop=True,
+            )
+            nc.vector.scalar_tensor_tensor(
+                out=y_t[k][:, j, :], in0=num[:], scalar=gam[:, 0:1], in1=r_t[k][:], op0=ALU.mult, op1=ALU.mult
+            )
+            adder = nc.vector if (u >= TICKS - TAIL_V and u % 2 == 1) else nc.gpsimd
+            adder.tensor_tensor(
+                out=y_t[k][:, j, :], in0=y_t[k][:, j, :], in1=x_sb[k // 2][:, j, (k % 2) * 512 : (k % 2) * 512 + 512],
+                op=ALU.add,
+            )
+            if k == CHUNKS - 1:
+                nc.sync.dma_start(out=out_v[b][:, j, cols], in_=y_t[k][:, j, :])
+            elif j == 3:
+                nc.sync.dma_start(out=out_v[b][:, :, cols], in_=y_t[k][:])
+
+        done = set()
+
+        def due(kind, t, lag, step, count):
+            idx, rem = divmod(t - lag, step)
+            if t < lag or rem != 0 or idx >= count or (kind, idx) in done:
+                return None
+            done.add((kind, idx))
+            return idx
+
+        def tick(t, fronts, with_back):
+            k = due("rc", t, LAG_RC, 4, fronts // 4)
+            if k is not None:
+                recip(k)
+            if t < fronts and ("f", t) not in done:
+                done.add(("f", t))
+                front(t)
+            if with_back and LAG_MX <= t < TICKS + LAG_MX:
+                back(t - LAG_MX)
+            k = due("q", t, LAG_Q, 4, fronts // 4)
+            if k is not None:
+                quantise_e(k)
+            pr = due("te", t, LAG_TE, 2, fronts // 2)
+            if pr is not None:
+                turn(pr)
+
+        for t in range(HEAD + LAG_Q - 3):
+            tick(t, HEAD, False)
+            if t == W3_AT:
+                prepare_w3()
+            if t == W3_AT + 1:
+                quantise_w3()
+            if t in X_AT:
+                regroup_x(X_AT[t], (RG0, RG1)[X_AT[t]])
+            if t == QX_AT:
+                quantise_x(0)
+        for g in range(NHALF):
+            pool_half(g)
+        nc.vector.tensor_copy(out=gam[:], in_=gam_bf[:])
+        for t in range(HEAD, TICKS + LAG_MX):
+            tick(t, TICKS, True)
+            if t == HEAD + 3:
+                quantise_c3p(B - 1)

@@ -24,16 +24,31 @@ TICKS = B * N // P
 CHUNKS = TICKS // 4
 LAG_TE = 3
 LAG_RC = 5
-LAG_Q = 6
-LAG_MX = 8
+LAG_Q = 7
+LAG_MX = 9
 HEAD = 8
 RG0 = "vvgg"
 RG1 = "vsgg"
 RGN = "sssg"
+RGE = "ssgg"
+C3_RING = 4
 TAIL_V = 8
 X_AT = {4: 0, 7: 1}
-QX_AT = 8
+QX_AT = 6
 W3_AT = 2
+HEAD_PLAN = {
+    2: [("w3",), ("qw3",), ("rg", 0, 3, "g")],
+    4: [("rg", 0, 1, "v")],
+    5: [("rg", 0, 2, "g"), ("rg", 1, 1, "s")],
+    6: [("rg", 0, 0, "v"), ("qx",)],
+    7: [("rg", 1, 0, "v")],
+    8: [("rg", 1, 2, "v"), ("rg", 1, 3, "s")],
+}
+AD_MOD = 1000
+QPOS = 1
+ADP = 4
+ADV = ()
+XG_BUFS = 2
 
 
 def tile_selfspatialattentionmodule_pb_t_kernel(tc, x, c2, c1p, W3, gamma, out):
@@ -111,11 +126,12 @@ def tile_selfspatialattentionmodule_pb_t_kernel(tc, x, c2, c1p, W3, gamma, out):
         xq_t = {}
         xs_t = {}
 
-        def regroup_x(g, engines):
-            xg = work.tile([P, 4, 256, 4], BF16, name="xg", tag="big", bufs=3, align_bytes=64)
-            xg_t[g] = xg
+        def regroup_x(g, engines, pieces=(0, 1, 2, 3)):
+            if g not in xg_t:
+                xg_t[g] = work.tile([P, 4, 256, 4], BF16, name="xg", bufs=XG_BUFS, align_bytes=64)
+            xg = xg_t[g]
             src = x_sb[g][:].rearrange("p j (i dh jj dw) -> p dh i jj dw j", i=16, dh=2, jj=16, dw=2)
-            for piece in range(4):
+            for piece in pieces:
                 dh, ih = divmod(piece, 2)
                 dst = xg[:, 2 * dh : 2 * dh + 2, P * ih : P * ih + P, :].rearrange("p dw (i jj) j -> p i jj dw j", i=8)
                 s = src[:, dh, 8 * ih : 8 * ih + 8]
@@ -157,14 +173,16 @@ def tile_selfspatialattentionmodule_pb_t_kernel(tc, x, c2, c1p, W3, gamma, out):
                 stop=stop,
             )
 
-        def pool_half(g):
+        def pool_half(g, vector_extras, pair):
             b, hf = divmod(g, 2)
+            if pair is not None:
+                turn_pe(pair)
             if hf == 0:
                 c3pb_t[b] = work.tile([P, 4, C], BF16, name="c3pb", tag="mid", bufs=3)
             acc = {}
             for mm in range(4):
                 for tl in range(2):
-                    c3 = bank(ring[0] % 6, [P, C], F32, "c3")
+                    c3 = bank(ring[0] % C3_RING, [P, C], F32, "c3")
                     ring[0] += 1
                     mx1(c3, g, mm, tl, True, True)
                     if mm == 0:
@@ -172,10 +190,17 @@ def tile_selfspatialattentionmodule_pb_t_kernel(tc, x, c2, c1p, W3, gamma, out):
                         nc.scalar.copy(out=acc[tl][:], in_=c3[:])
                     else:
                         nc.vector.tensor_tensor(out=acc[tl][:], in0=acc[tl][:], in1=c3[:], op=ALU.max)
+                if mm == 0 and pair is not None:
+                    turn_s(pair)
+                if mm == 0 and g == 0:
+                    for act in HEAD_PLAN.get(HEAD, ()):
+                        regroup_x(act[1], {act[2]: act[3]}, (act[2],))
             if g + 1 < NHALF:
                 quantise_x(g + 1)
             if hf == 0 and b > 0:
                 quantise_c3p(b - 1)
+            for extra in vector_extras:
+                extra[0](extra[1])
             for tl in range(2):
                 tot = bank(6 + tl, [P, C], F32, "tot")
                 for mm in range(4):
@@ -184,7 +209,7 @@ def tile_selfspatialattentionmodule_pb_t_kernel(tc, x, c2, c1p, W3, gamma, out):
                     out=c3pb_t[b][:, 2 * hf + tl, :], in0=tot[:], scalar=0.25, in1=acc[tl][:], op0=ALU.mult, op1=ALU.add
                 )
             if g + 2 < NHALF:
-                regroup_x(g + 2, RGN)
+                regroup_x(g + 2, RGE if g < 4 else RGN)
             if hf == 1:
                 c3g_t[b] = work.tile([P, C, 4], BF16, name="c3g", tag="grp", bufs=2, align_bytes=64)
                 nc.gpsimd.tensor_scalar(
@@ -233,33 +258,46 @@ def tile_selfspatialattentionmodule_pb_t_kernel(tc, x, c2, c1p, W3, gamma, out):
                 out=eq_t[k][:].bitcast(FP8X4), scales=es_t[k][:], in_=eg_t[k][:].rearrange("p n t -> p (n t)")
             )
 
-        def turn(pr):
+        tr_t = {}
+
+        def turn_pe(pr):
             k, half = divmod(pr, 2)
-            if half == 0:
-                eg_t[k] = work.tile([P, 512, 4], BF16, name="eg", tag="grp", bufs=2, align_bytes=64)
-            e_tr = bank(5 + pr % 2, [P, 2, 4, P], BF16, "e_tr")
+            early = pr < HEAD // 2
+            e_tr = bank((4 if early else 5) + pr % 2, [P, 2, 4, P], BF16, "e_tr")
+            tr_t[pr] = e_tr
             for i2 in range(2):
                 for tt in range(4):
                     nc.tensor.transpose(e_tr[:, i2, tt, :], e_t[k][:, 2 * half + i2, tt * P : tt * P + P], ident_b[:])
-            nc.scalar.copy(
-                out=eg_t[k][:, 256 * half : 256 * half + 256, :].rearrange("p (i n) t -> p i n t", i=2),
-                in_=e_tr[:].rearrange("p i t n -> p i n t"),
-            )
             if half == 1:
-                r_ps = bank(7, [P, 512], F32, "r_ps")
+                r_ps = bank(4 if early else 7, [P, 512], F32, "r_ps")
+                tr_t["r", k] = r_ps
                 for i in range(4):
                     nc.tensor.transpose(
                         r_ps[:, i * P : i * P + P], rcp_t[k][:, i : i + 1].to_broadcast([P, P]), ident_f[:]
                     )
+
+        def turn_s(pr):
+            k, half = divmod(pr, 2)
+            if half == 0:
+                eg_t[k] = work.tile([P, 512, 4], BF16, name="eg", tag="grp", bufs=2, align_bytes=64)
+            nc.scalar.copy(
+                out=eg_t[k][:, 256 * half : 256 * half + 256, :].rearrange("p (i n) t -> p i n t", i=2),
+                in_=tr_t[pr][:].rearrange("p i t n -> p i n t"),
+            )
+            if half == 1:
                 r_t[k] = work.tile([P, 512], F32, name="r_sb", bufs=3)
-                nc.scalar.copy(out=r_t[k][:], in_=r_ps[:])
+                nc.scalar.copy(out=r_t[k][:], in_=tr_t["r", k][:])
+
+        def turn(pr):
+            turn_pe(pr)
+            turn_s(pr)
 
         def back(u):
             k, j = divmod(u, 4)
             b = k // 4
             cols = slice((k % 4) * 512, (k % 4) * 512 + 512)
             if j == 0:
-                y_t[k] = work.tile([P, 4, 512], F32, name="y", tag="big", bufs=3, align_bytes=64)
+                y_t[k] = work.tile([P, 4, 512], F32, name="y", bufs=3)
             num = bank(3 + u % 2, [P, 512], F32, "num")
             nc.tensor.matmul_mx(
                 out=num[:],
@@ -273,7 +311,7 @@ def tile_selfspatialattentionmodule_pb_t_kernel(tc, x, c2, c1p, W3, gamma, out):
             nc.vector.scalar_tensor_tensor(
                 out=y_t[k][:, j, :], in0=num[:], scalar=gam[:, 0:1], in1=r_t[k][:], op0=ALU.mult, op1=ALU.mult
             )
-            adder = nc.vector if (u >= TICKS - TAIL_V and u % 2 == 1) else nc.gpsimd
+            adder = nc.vector if ((u >= TICKS - TAIL_V and u % 2 == 1) or (u % ADP in ADV)) else nc.gpsimd
             adder.tensor_tensor(
                 out=y_t[k][:, j, :], in0=y_t[k][:, j, :], in1=x_sb[k // 2][:, j, (k % 2) * 512 : (k % 2) * 512 + 512],
                 op=ALU.add,
@@ -299,27 +337,40 @@ def tile_selfspatialattentionmodule_pb_t_kernel(tc, x, c2, c1p, W3, gamma, out):
             if t < fronts and ("f", t) not in done:
                 done.add(("f", t))
                 front(t)
+            if QPOS == 0:
+                k = due("q", t, LAG_Q, 4, fronts // 4)
+                if k is not None:
+                    quantise_e(k)
             if with_back and LAG_MX <= t < TICKS + LAG_MX:
                 back(t - LAG_MX)
-            k = due("q", t, LAG_Q, 4, fronts // 4)
-            if k is not None:
-                quantise_e(k)
+            if QPOS == 1:
+                k = due("q", t, LAG_Q, 4, fronts // 4)
+                if k is not None:
+                    quantise_e(k)
             pr = due("te", t, LAG_TE, 2, fronts // 2)
             if pr is not None:
                 turn(pr)
 
-        for t in range(HEAD + LAG_Q - 3):
-            tick(t, HEAD, False)
-            if t == W3_AT:
-                prepare_w3()
-            if t == W3_AT + 1:
-                quantise_w3()
-            if t in X_AT:
-                regroup_x(X_AT[t], (RG0, RG1)[X_AT[t]])
-            if t == QX_AT:
-                quantise_x(0)
+        for t in range(HEAD):
+            done.add(("f", t))
+            front(t)
+            for act in HEAD_PLAN.get(t, ()):
+                if act[0] == "w3":
+                    prepare_w3()
+                elif act[0] == "qw3":
+                    quantise_w3()
+                elif act[0] == "qx":
+                    quantise_x(0)
+                else:
+                    regroup_x(act[1], {act[2]: act[3]}, (act[2],))
+        for k in range(HEAD // 4):
+            done.add(("rc", k))
+            done.add(("q", k))
+            done.add(("te", 2 * k))
+            done.add(("te", 2 * k + 1))
+        vector_extras = {0: [(recip, 0)], 2: [(quantise_e, 0), (recip, 1)], 4: [(quantise_e, 1)]}
         for g in range(NHALF):
-            pool_half(g)
+            pool_half(g, vector_extras.get(g, []), g if g < HEAD // 2 else None)
         nc.vector.tensor_copy(out=gam[:], in_=gam_bf[:])
         for t in range(HEAD, TICKS + LAG_MX):
             tick(t, TICKS, True)

@@ -54,7 +54,6 @@ XG_BUFS = 2
 def tile_selfspatialattentionmodule_pb_t_kernel(tc, x, c2, c1p, W3, gamma, out):
     nc = tc.nc
     with ExitStack() as ctx:
-        ctx.enter_context(tc.manual_schedule())
         keep = ctx.enter_context(tc.tile_pool(name="keep", bufs=1))
         work = ctx.enter_context(tc.tile_pool(name="work", bufs=2))
         psum = ctx.enter_context(tc.psum_pool(name="psum", bufs=1))

@@ -49,6 +49,7 @@ QPOS = 1
 ADP = 4
 ADV = ()
 XG_BUFS = 2
+GRP_BUFS = 3
 
 
 def tile_selfspatialattentionmodule_pb_t_kernel(tc, x, c2, c1p, W3, gamma, out):
@@ -127,7 +128,7 @@ def tile_selfspatialattentionmodule_pb_t_kernel(tc, x, c2, c1p, W3, gamma, out):
 
         def regroup_x(g, engines, pieces=(0, 1, 2, 3)):
             if g not in xg_t:
-                xg_t[g] = work.tile([P, 4, 256, 4], BF16, name="xg", bufs=XG_BUFS, align_bytes=64)
+                xg_t[g] = work.tile([P, 4, 256, 4], BF16, name="xg", tag="big", bufs=3, align_bytes=64)
             xg = xg_t[g]
             src = x_sb[g][:].rearrange("p j (i dh jj dw) -> p dh i jj dw j", i=16, dh=2, jj=16, dw=2)
             for piece in pieces:
@@ -177,7 +178,7 @@ def tile_selfspatialattentionmodule_pb_t_kernel(tc, x, c2, c1p, W3, gamma, out):
             if pair is not None:
                 turn_pe(pair)
             if hf == 0:
-                c3pb_t[b] = work.tile([P, 4, C], BF16, name="c3pb", tag="mid", bufs=3)
+                c3g_t[b] = work.tile([P, C, 4], BF16, name="c3g", bufs=2, align_bytes=64)
             acc = {}
             for mm in range(4):
                 for tl in range(2):
@@ -204,17 +205,11 @@ def tile_selfspatialattentionmodule_pb_t_kernel(tc, x, c2, c1p, W3, gamma, out):
                 tot = bank(6 + tl, [P, C], F32, "tot")
                 for mm in range(4):
                     mx1(tot, g, mm, tl, mm == 0, mm == 3)
-                nc.vector.scalar_tensor_tensor(
-                    out=c3pb_t[b][:, 2 * hf + tl, :], in0=tot[:], scalar=0.25, in1=acc[tl][:], op0=ALU.mult, op1=ALU.add
-                )
+                mean = work.tile([P, C], F32, name="mean%d" % tl)
+                nc.scalar.mul(out=mean[:], in_=tot[:], mul=0.25)
+                nc.gpsimd.tensor_tensor(out=c3g_t[b][:, :, 2 * hf + tl], in0=acc[tl][:], in1=mean[:], op=ALU.add)
             if g + 2 < NHALF:
                 regroup_x(g + 2, RGE if g < 4 else RGN)
-            if hf == 1:
-                c3g_t[b] = work.tile([P, C, 4], BF16, name="c3g", tag="grp", bufs=2, align_bytes=64)
-                nc.gpsimd.tensor_scalar(
-                    out=c3g_t[b][:], in0=c3pb_t[b][:].rearrange("p t c -> p c t"), scalar1=1.0, scalar2=0.0,
-                    op0=ALU.mult, op1=ALU.add,
-                )
 
         nmx_t = {}
         sum_t = {}
@@ -278,7 +273,7 @@ def tile_selfspatialattentionmodule_pb_t_kernel(tc, x, c2, c1p, W3, gamma, out):
         def turn_s(pr):
             k, half = divmod(pr, 2)
             if half == 0:
-                eg_t[k] = work.tile([P, 512, 4], BF16, name="eg", tag="grp", bufs=2, align_bytes=64)
+                eg_t[k] = work.tile([P, 512, 4], BF16, name="eg", bufs=2, align_bytes=64)
             nc.scalar.copy(
                 out=eg_t[k][:, 256 * half : 256 * half + 256, :].rearrange("p (i n) t -> p i n t", i=2),
                 in_=tr_t[pr][:].rearrange("p i t n -> p i n t"),
@@ -296,7 +291,7 @@ def tile_selfspatialattentionmodule_pb_t_kernel(tc, x, c2, c1p, W3, gamma, out):
             b = k // 4
             cols = slice((k % 4) * 512, (k % 4) * 512 + 512)
             if j == 0:
-                y_t[k] = work.tile([P, 4, 512], F32, name="y", bufs=3)
+                y_t[k] = work.tile([P, 4, 512], F32, name="y", tag="big", bufs=3, align_bytes=64)
             num = bank(3 + u % 2, [P, 512], F32, "num")
             nc.tensor.matmul_mx(
                 out=num[:],

@@ -16,40 +16,39 @@ B, C, H, W = 4, 512, 64, 32
 CH = C // 2
 N = H * W
 M = (H // 2) * (W // 2)
-P = 128
 FLOPS = 2 * B * (C * C * N + CH * N * M + C * M * N)
 
-NHALF = 2 * B
-TICKS = B * N // P
-CHUNKS = TICKS // 4
-LAG_TE = 3
-LAG_RC = 5
-LAG_Q = 7
-LAG_MX = 9
-HEAD = 8
-RG0 = "vvgg"
-RG1 = "vsgg"
-RGN = "sssg"
-RGE = "ssgg"
-C3_RING = 4
-TAIL_V = 8
-X_AT = {4: 0, 7: 1}
-QX_AT = 6
-W3_AT = 2
-HEAD_PLAN = {
-    2: [("w3",), ("qw3",), ("rg", 0, 3, "g")],
-    4: [("rg", 0, 1, "v")],
-    5: [("rg", 0, 2, "g"), ("rg", 1, 1, "s")],
-    6: [("rg", 0, 0, "v"), ("qx",)],
-    7: [("rg", 1, 0, "v")],
-    8: [("rg", 1, 2, "v"), ("rg", 1, 3, "s")],
-}
-AD_MOD = 1000
-QPOS = 1
-ADP = 4
-ADV = ()
-XG_BUFS = 2
-GRP_BUFS = 3
+P = 128
+PACK = 4
+HALF = N // 2
+HALVES = 2 * B
+POOLED = HALF // 4
+CHUNK = 4 * P
+TILES = B * N // P
+CHUNKS = TILES // 4
+EARLY_CHUNKS = 2
+EARLY_TILES = 4 * EARLY_CHUNKS
+
+TURN_LAG = 3
+RECIPROCAL_LAG = 5
+QUANTISE_LAG = 7
+PRODUCT_LAG = 9
+SHARED_ADDS = 8
+IN_FLIGHT = 3
+
+W3_BANKS = (3, 4)
+C3_BANKS = (0, 1, 2, 3)
+EARLY_TURN_BANKS = (4, 5)
+SUM_BANKS = (6, 7)
+SCORE_BANKS = (0, 1, 2)
+PRODUCT_BANKS = (3, 4)
+TURN_BANKS = (5, 6)
+SPREAD_BANK = 7
+
+REGROUP_HALF_0 = "vvgg"
+REGROUP_HALF_1 = "vsvs"
+REGROUP_BESIDE_TURNS = "ssgg"
+REGROUP_LATER = "sssg"
 
 
 def tile_selfspatialattentionmodule_pb_t_kernel(tc, x, c2, c1p, W3, gamma, out):
@@ -59,314 +58,323 @@ def tile_selfspatialattentionmodule_pb_t_kernel(tc, x, c2, c1p, W3, gamma, out):
         work = ctx.enter_context(tc.tile_pool(name="work", bufs=2))
         psum = ctx.enter_context(tc.psum_pool(name="psum", bufs=1))
 
-        def bank(idx, shape, dtype, name):
-            return psum.tile(shape, dtype, name=name, tag="bank%d" % idx)
+        def psum_bank(index, shape, dtype, name):
+            return psum.tile(shape, dtype, name=name, tag="bank%d" % index)
 
-        x_sb = [keep.tile([P, 4, N // 2], BF16, name="x_sb%d" % g) for g in range(NHALF)]
-        c2_sb = [keep.tile([P, 2, N // 2], BF16, name="c2_sb%d" % g) for g in range(NHALF)]
+        x_sb = [keep.tile([P, PACK, HALF], BF16, name="x_sb%d" % g) for g in range(HALVES)]
+        c2_sb = [keep.tile([P, 2, HALF], BF16, name="c2_sb%d" % g) for g in range(HALVES)]
         c1_sb = [keep.tile([P, 2, M], BF16, name="c1_sb%d" % b) for b in range(B)]
-        w3_sb = keep.tile([P, 4, C], BF16, name="w3_sb")
-        gam_bf = keep.tile([P, 1], BF16, name="gam_bf")
+        w3_sb = keep.tile([P, PACK, C], BF16, name="w3_sb")
+        gamma_bf = keep.tile([P, 1], BF16, name="gamma_bf")
+
+        def pixels_of_half(g):
+            return slice((g % 2) * HALF, (g % 2 + 1) * HALF)
 
         def load_x(g):
-            cols = slice((g % 2) * (N // 2), (g % 2 + 1) * (N // 2))
-            nc.sync.dma_start(out=x_sb[g][:], in_=x[g // 2].rearrange("(p j) h w -> p j (h w)", j=4)[:, :, cols])
+            view = x[g // 2].rearrange("(p j) h w -> p j (h w)", j=PACK)
+            nc.sync.dma_start(out=x_sb[g][:], in_=view[:, :, pixels_of_half(g)])
 
         def load_c2(g):
-            cols = slice((g % 2) * (N // 2), (g % 2 + 1) * (N // 2))
-            nc.sync.dma_start(out=c2_sb[g][:], in_=c2[g // 2].rearrange("(g p) h w -> p g (h w)", g=2)[:, :, cols])
+            view = c2[g // 2].rearrange("(u p) h w -> p u (h w)", u=2)
+            nc.sync.dma_start(out=c2_sb[g][:], in_=view[:, :, pixels_of_half(g)])
 
         def load_c1(b):
-            nc.sync.dma_start(out=c1_sb[b][:], in_=c1p[b].rearrange("(g p) i j -> p g (i j)", g=2))
+            nc.sync.dma_start(out=c1_sb[b][:], in_=c1p[b].rearrange("(u p) i j -> p u (i j)", u=2))
 
         load_c1(0)
         load_c2(0)
-        nc.sync.dma_start(out=w3_sb[:], in_=W3.rearrange("(p a) i -> p a i", a=4))
-        for g in range(NHALF):
+        nc.sync.dma_start(out=w3_sb[:], in_=W3.rearrange("(p a) i -> p a i", a=PACK))
+        for g in range(HALVES):
             load_x(g)
-        nc.sync.dma_start(out=gam_bf[:], in_=gamma.partition_broadcast(P))
+        nc.sync.dma_start(out=gamma_bf[:], in_=gamma.partition_broadcast(P))
         load_c2(1)
         for b in range(1, B):
             load_c1(b)
             load_c2(2 * b)
             load_c2(2 * b + 1)
 
-        ident_b = keep.tile([P, P], BF16, name="ident_b")
-        make_identity(nc, ident_b[:])
-        ident_f = keep.tile([P, P], F32, name="ident_f")
-        make_identity(nc, ident_f[:])
+        ident_bf = keep.tile([P, P], BF16, name="ident_bf")
+        make_identity(nc, ident_bf[:])
+        ident_f32 = keep.tile([P, P], F32, name="ident_f32")
+        make_identity(nc, ident_f32[:])
         warm_in = keep.tile([P, 1], F32, name="warm_in")
         warm_out = keep.tile([P, 1], F32, name="warm_out")
         nc.vector.memset(warm_in[:], 0.0)
         nc.scalar.activation(out=warm_out[:], in_=warm_in[:], func=ACT.Exp)
+        gamma_f32 = keep.tile([P, 1], F32, name="gamma_f32")
 
-        w3_g = keep.tile([P, C, 4], BF16, name="w3_g", align_bytes=64)
-        w3_q = keep.tile([P, C], U32, name="w3_q", align_bytes=64)
-        w3_s = keep.tile([P, C], U8, name="w3_s", align_bytes=64)
+        def copy_on(engine, dst, src):
+            if engine == "v":
+                nc.vector.tensor_copy(out=dst, in_=src)
+            elif engine == "s":
+                nc.scalar.copy(out=dst, in_=src)
+            else:
+                nc.gpsimd.tensor_scalar(out=dst, in0=src, scalar1=1.0, scalar2=0.0, op0=ALU.mult, op1=ALU.add)
 
-        def prepare_w3():
-            w3_words = w3_sb[:].bitcast(F32).rearrange("p a (q u) -> p a u q", u=2)
-            w3_g32 = w3_g[:].bitcast(F32)
+        w3_grouped = keep.tile([P, C, PACK], BF16, name="w3_grouped", align_bytes=64)
+        w3_words = keep.tile([P, C], U32, name="w3_words", align_bytes=64)
+        w3_scales = keep.tile([P, C], U8, name="w3_scales", align_bytes=64)
+
+        def transpose_w3():
+            pairs = w3_sb[:].bitcast(F32).rearrange("p a (q u) -> p a u q", u=2)
+            grouped_pairs = w3_grouped[:].bitcast(F32)
             for h in range(2):
-                w_t = bank(3 + h, [P, 2, 2, P], F32, "w_t")
+                turned = psum_bank(W3_BANKS[h], [P, 2, 2, P], F32, "w3_turned")
                 for u in range(2):
                     for a in range(2):
-                        nc.tensor.transpose(w_t[:, u, a, :], w3_words[:, 2 * h + a, u, :], ident_f[:])
+                        nc.tensor.transpose(turned[:, u, a, :], pairs[:, 2 * h + a, u, :], ident_f32[:])
                 nc.vector.tensor_copy(
-                    out=w3_g32[:, 256 * h : 256 * h + 256, :].rearrange("p (a q) u -> p a q u", a=2),
-                    in_=w_t[:].rearrange("p u a q -> p a q u"),
+                    out=grouped_pairs[:, 2 * P * h : 2 * P * (h + 1), :].rearrange("p (a q) u -> p a q u", a=2),
+                    in_=turned[:].rearrange("p u a q -> p a q u"),
                 )
 
         def quantise_w3():
             nc.vector.quantize_mx(
-                out=w3_q[:].bitcast(FP8X4), scales=w3_s[:], in_=w3_g[:].rearrange("p c t -> p (c t)")
+                out=w3_words[:].bitcast(FP8X4), scales=w3_scales[:], in_=w3_grouped[:].rearrange("p c j -> p (c j)")
             )
 
-        xg_t = {}
-        xq_t = {}
-        xs_t = {}
+        x_grouped = {}
+        x_words = {}
+        x_scales = {}
 
-        def regroup_x(g, engines, pieces=(0, 1, 2, 3)):
-            if g not in xg_t:
-                xg_t[g] = work.tile([P, 4, 256, 4], BF16, name="xg", tag="big", bufs=3, align_bytes=64)
-            xg = xg_t[g]
+        def regroup_x(g, engines):
+            x_grouped[g] = work.tile([P, 4, POOLED, PACK], BF16, name="x_grouped", align_bytes=64)
             src = x_sb[g][:].rearrange("p j (i dh jj dw) -> p dh i jj dw j", i=16, dh=2, jj=16, dw=2)
-            for piece in pieces:
-                dh, ih = divmod(piece, 2)
-                dst = xg[:, 2 * dh : 2 * dh + 2, P * ih : P * ih + P, :].rearrange("p dw (i jj) j -> p i jj dw j", i=8)
-                s = src[:, dh, 8 * ih : 8 * ih + 8]
-                eng = engines[piece]
-                if eng == "v":
-                    nc.vector.tensor_copy(out=dst, in_=s)
-                elif eng == "s":
-                    nc.scalar.copy(out=dst, in_=s)
-                else:
-                    nc.gpsimd.tensor_scalar(out=dst, in0=s, scalar1=1.0, scalar2=0.0, op0=ALU.mult, op1=ALU.add)
+            for piece in range(4):
+                dh, rows = divmod(piece, 2)
+                dst = x_grouped[g][:, 2 * dh : 2 * dh + 2, P * rows : P * (rows + 1), :]
+                copy_on(
+                    engines[piece],
+                    dst.rearrange("p dw (i jj) j -> p i jj dw j", i=8),
+                    src[:, dh, 8 * rows : 8 * (rows + 1)],
+                )
 
         def quantise_x(g):
-            xq_t[g] = work.tile([P, 1024], U32, name="xq", align_bytes=64)
-            xs_t[g] = work.tile([P, 1024], U8, name="xs", align_bytes=64)
+            x_words[g] = work.tile([P, 4 * POOLED], U32, name="x_words", align_bytes=64)
+            x_scales[g] = work.tile([P, 4 * POOLED], U8, name="x_scales", align_bytes=64)
             nc.vector.quantize_mx(
-                out=xq_t[g][:].bitcast(FP8X4), scales=xs_t[g][:], in_=xg_t[g][:].rearrange("p m q j -> p (m q j)")
+                out=x_words[g][:].bitcast(FP8X4),
+                scales=x_scales[g][:],
+                in_=x_grouped[g][:].rearrange("p m q j -> p (m q j)"),
             )
 
-        c3q = [keep.tile([P, C], U32, name="c3q%d" % b, align_bytes=64) for b in range(B)]
-        c3s = [keep.tile([P, C], U8, name="c3s%d" % b, align_bytes=64) for b in range(B)]
-        c3pb_t = {}
-        c3g_t = {}
-        ring = [0]
+        c3p_words = [keep.tile([P, C], U32, name="c3p_words%d" % b, align_bytes=64) for b in range(B)]
+        c3p_scales = [keep.tile([P, C], U8, name="c3p_scales%d" % b, align_bytes=64) for b in range(B)]
+        c3p_planes = {}
+        c3p_grouped = {}
+        c3_count = [0]
 
-        def quantise_c3p(b):
-            nc.vector.quantize_mx(
-                out=c3q[b][:].bitcast(FP8X4), scales=c3s[b][:], in_=c3g_t[b][:].rearrange("p c t -> p (c t)")
-            )
-
-        def mx1(dst, g, mm, tl, start, stop):
-            cols = slice(mm * 256 + tl * P, mm * 256 + tl * P + P)
+        def step_1_pass(dst, g, member, part, start, stop):
+            cols = slice(member * POOLED + part * P, member * POOLED + (part + 1) * P)
             nc.tensor.matmul_mx(
                 out=dst[:],
-                lhsT=xq_t[g][:, cols].bitcast(FP8X4),
-                lhsT_scale=xs_t[g][:, cols],
-                rhs=w3_q[:].bitcast(FP8X4),
-                rhs_scale=w3_s[:],
+                lhsT=x_words[g][:, cols].bitcast(FP8X4),
+                lhsT_scale=x_scales[g][:, cols],
+                rhs=w3_words[:].bitcast(FP8X4),
+                rhs_scale=w3_scales[:],
                 start=start,
                 stop=stop,
             )
 
-        def pool_half(g, vector_extras, pair):
-            b, hf = divmod(g, 2)
-            if pair is not None:
-                turn_pe(pair)
-            if hf == 0:
-                c3g_t[b] = work.tile([P, C, 4], BF16, name="c3g", bufs=2, align_bytes=64)
-            acc = {}
-            for mm in range(4):
-                for tl in range(2):
-                    c3 = bank(ring[0] % C3_RING, [P, C], F32, "c3")
-                    ring[0] += 1
-                    mx1(c3, g, mm, tl, True, True)
-                    if mm == 0:
-                        acc[tl] = work.tile([P, C], F32, name="acc%d" % tl)
-                        nc.scalar.copy(out=acc[tl][:], in_=c3[:])
-                    else:
-                        nc.vector.tensor_tensor(out=acc[tl][:], in0=acc[tl][:], in1=c3[:], op=ALU.max)
-                if mm == 0 and pair is not None:
-                    turn_s(pair)
-                if mm == 0 and g == 0:
-                    for act in HEAD_PLAN.get(HEAD, ()):
-                        regroup_x(act[1], {act[2]: act[3]}, (act[2],))
-            if g + 1 < NHALF:
-                quantise_x(g + 1)
-            if hf == 0 and b > 0:
-                quantise_c3p(b - 1)
-            for extra in vector_extras:
-                extra[0](extra[1])
-            for tl in range(2):
-                tot = bank(6 + tl, [P, C], F32, "tot")
-                for mm in range(4):
-                    mx1(tot, g, mm, tl, mm == 0, mm == 3)
-                mean = work.tile([P, C], F32, name="mean%d" % tl)
-                nc.scalar.mul(out=mean[:], in_=tot[:], mul=0.25)
-                nc.gpsimd.tensor_tensor(out=c3g_t[b][:, :, 2 * hf + tl], in0=acc[tl][:], in1=mean[:], op=ALU.add)
-            if g + 2 < NHALF:
-                regroup_x(g + 2, RGE if g < 4 else RGN)
-
-        nmx_t = {}
-        sum_t = {}
-        e_t = {}
-        eg_t = {}
-        eq_t = {}
-        es_t = {}
-        rcp_t = {}
-        r_t = {}
-        y_t = {}
-        gam = keep.tile([P, 1], F32, name="gam")
-        out_v = [out[b].rearrange("(p j) h w -> p j (h w)", j=4) for b in range(B)]
-
-        def front(t):
-            k, i = divmod(t, 4)
-            n0 = (k % 2) * 512 + i * P
-            if i == 0:
-                nmx_t[k] = work.tile([P, 4], F32, name="nmx", bufs=3)
-                sum_t[k] = work.tile([P, 4], F32, name="sums", bufs=3)
-                e_t[k] = work.tile([P, 4, M], BF16, name="e_bf", tag="mid", bufs=3)
-            sc = bank(t % 3, [P, M], F32, "sc")
-            for h in range(2):
-                nc.tensor.matmul(
-                    out=sc[:], lhsT=c2_sb[k // 2][:, h, n0 : n0 + P], rhs=c1_sb[k // 4][:, h, :], start=h == 0, stop=h == 1
-                )
-            nc.vector.tensor_reduce(out=nmx_t[k][:, i : i + 1], in_=sc[:], axis=AX.X, op=ALU.max, negate=True)
-            nc.scalar.activation(
-                out=e_t[k][:, i, :], in_=sc[:], func=ACT.Exp, bias=nmx_t[k][:, i : i + 1], scale=1.0,
-                accum_out=sum_t[k][:, i : i + 1],
-            )
-
-        def recip(k):
-            rcp_t[k] = work.tile([P, 4], F32, name="rcp", bufs=2)
-            nc.vector.reciprocal(out=rcp_t[k][:], in_=sum_t[k][:])
-
-        def quantise_e(k):
-            eq_t[k] = work.tile([P, 512], U32, name="eq", bufs=3, align_bytes=64)
-            es_t[k] = work.tile([P, 512], U8, name="es", bufs=3, align_bytes=64)
+        def quantise_c3p(b):
             nc.vector.quantize_mx(
-                out=eq_t[k][:].bitcast(FP8X4), scales=es_t[k][:], in_=eg_t[k][:].rearrange("p n t -> p (n t)")
+                out=c3p_words[b][:].bitcast(FP8X4),
+                scales=c3p_scales[b][:],
+                in_=c3p_grouped[b][:].rearrange("p c t -> p (c t)"),
             )
 
-        tr_t = {}
+        def pool_half(g):
+            b, second = divmod(g, 2)
+            early_pair = g if g < EARLY_TILES // 2 else None
+            if early_pair is not None:
+                transpose_pair(early_pair)
+            if not second:
+                c3p_planes[b] = work.tile([P, PACK, C], BF16, name="c3p_planes", tag="four_planes", bufs=IN_FLIGHT)
+            largest = {}
+            for member in range(4):
+                for part in range(2):
+                    c3 = psum_bank(C3_BANKS[c3_count[0] % len(C3_BANKS)], [P, C], F32, "c3")
+                    c3_count[0] += 1
+                    step_1_pass(c3, g, member, part, True, True)
+                    if member == 0:
+                        largest[part] = work.tile([P, C], F32, name="largest%d" % part)
+                        nc.scalar.copy(out=largest[part][:], in_=c3[:])
+                    else:
+                        nc.vector.tensor_tensor(out=largest[part][:], in0=largest[part][:], in1=c3[:], op=ALU.max)
+                if member == 0 and early_pair is not None:
+                    copy_pair(early_pair)
+            if g + 1 < HALVES:
+                quantise_x(g + 1)
+            if not second and b > 0:
+                quantise_c3p(b - 1)
+            if not second and 0 < b <= EARLY_CHUNKS:
+                quantise_e(b - 1)
+            if not second and b < EARLY_CHUNKS:
+                reciprocal_of_sums(b)
+            for part in range(2):
+                total = psum_bank(SUM_BANKS[part], [P, C], F32, "total")
+                for member in range(4):
+                    step_1_pass(total, g, member, part, member == 0, member == 3)
+                nc.vector.scalar_tensor_tensor(
+                    out=c3p_planes[b][:, 2 * second + part, :],
+                    in0=total[:],
+                    scalar=0.25,
+                    in1=largest[part][:],
+                    op0=ALU.mult,
+                    op1=ALU.add,
+                )
+            if g + 2 < HALVES:
+                regroup_x(g + 2, REGROUP_BESIDE_TURNS if early_pair is not None else REGROUP_LATER)
+            if second:
+                c3p_grouped[b] = work.tile([P, C, PACK], BF16, name="c3p_grouped", tag="grouped", bufs=2, align_bytes=64)
+                copy_on("g", c3p_grouped[b][:], c3p_planes[b][:].rearrange("p t c -> p c t"))
 
-        def turn_pe(pr):
-            k, half = divmod(pr, 2)
-            early = pr < HEAD // 2
-            e_tr = bank((4 if early else 5) + pr % 2, [P, 2, 4, P], BF16, "e_tr")
-            tr_t[pr] = e_tr
-            for i2 in range(2):
-                for tt in range(4):
-                    nc.tensor.transpose(e_tr[:, i2, tt, :], e_t[k][:, 2 * half + i2, tt * P : tt * P + P], ident_b[:])
-            if half == 1:
-                r_ps = bank(4 if early else 7, [P, 512], F32, "r_ps")
-                tr_t["r", k] = r_ps
+        negative_max = {}
+        sums = {}
+        e_bf = {}
+        e_turned = {}
+        e_grouped = {}
+        e_words = {}
+        e_scales = {}
+        reciprocals = {}
+        spread_psum = {}
+        spread = {}
+        result = {}
+        out_view = [out[b].rearrange("(p j) h w -> p j (h w)", j=PACK) for b in range(B)]
+
+        def scores_and_exponentials(t):
+            k, i = divmod(t, 4)
+            first = (k % 2) * CHUNK + i * P
+            if i == 0:
+                negative_max[k] = work.tile([P, 4], F32, name="negative_max", bufs=IN_FLIGHT)
+                sums[k] = work.tile([P, 4], F32, name="sums", bufs=IN_FLIGHT)
+                e_bf[k] = work.tile([P, 4, M], BF16, name="e_bf", tag="four_planes", bufs=IN_FLIGHT)
+            scores = psum_bank(SCORE_BANKS[t % len(SCORE_BANKS)], [P, M], F32, "scores")
+            for u in range(2):
+                nc.tensor.matmul(
+                    out=scores[:],
+                    lhsT=c2_sb[k // 2][:, u, first : first + P],
+                    rhs=c1_sb[k // 4][:, u, :],
+                    start=u == 0,
+                    stop=u == 1,
+                )
+            nc.vector.tensor_reduce(
+                out=negative_max[k][:, i : i + 1], in_=scores[:], axis=AX.X, op=ALU.max, negate=True
+            )
+            nc.scalar.activation(
+                out=e_bf[k][:, i, :],
+                in_=scores[:],
+                func=ACT.Exp,
+                bias=negative_max[k][:, i : i + 1],
+                scale=1.0,
+                accum_out=sums[k][:, i : i + 1],
+            )
+
+        def reciprocal_of_sums(k):
+            reciprocals[k] = work.tile([P, 4], F32, name="reciprocals")
+            nc.vector.reciprocal(out=reciprocals[k][:], in_=sums[k][:])
+
+        def transpose_pair(pair):
+            k, second = divmod(pair, 2)
+            early = pair < EARLY_TILES // 2
+            banks = EARLY_TURN_BANKS if early else TURN_BANKS
+            e_turned[pair] = psum_bank(banks[pair % 2], [P, 2, PACK, P], BF16, "e_turned")
+            for i in range(2):
+                for t in range(PACK):
+                    nc.tensor.transpose(
+                        e_turned[pair][:, i, t, :], e_bf[k][:, 2 * second + i, t * P : (t + 1) * P], ident_bf[:]
+                    )
+            if second:
+                spread_psum[k] = psum_bank(EARLY_TURN_BANKS[0] if early else SPREAD_BANK, [P, CHUNK], F32, "spread_psum")
                 for i in range(4):
                     nc.tensor.transpose(
-                        r_ps[:, i * P : i * P + P], rcp_t[k][:, i : i + 1].to_broadcast([P, P]), ident_f[:]
+                        spread_psum[k][:, i * P : (i + 1) * P],
+                        reciprocals[k][:, i : i + 1].to_broadcast([P, P]),
+                        ident_f32[:],
                     )
 
-        def turn_s(pr):
-            k, half = divmod(pr, 2)
-            if half == 0:
-                eg_t[k] = work.tile([P, 512, 4], BF16, name="eg", bufs=2, align_bytes=64)
+        def copy_pair(pair):
+            k, second = divmod(pair, 2)
+            if not second:
+                e_grouped[k] = work.tile([P, CHUNK, PACK], BF16, name="e_grouped", tag="grouped", bufs=2, align_bytes=64)
             nc.scalar.copy(
-                out=eg_t[k][:, 256 * half : 256 * half + 256, :].rearrange("p (i n) t -> p i n t", i=2),
-                in_=tr_t[pr][:].rearrange("p i t n -> p i n t"),
+                out=e_grouped[k][:, 2 * P * second : 2 * P * (second + 1), :].rearrange("p (i n) t -> p i n t", i=2),
+                in_=e_turned[pair][:].rearrange("p i t n -> p i n t"),
             )
-            if half == 1:
-                r_t[k] = work.tile([P, 512], F32, name="r_sb", bufs=3)
-                nc.scalar.copy(out=r_t[k][:], in_=tr_t["r", k][:])
+            if second:
+                spread[k] = work.tile([P, CHUNK], F32, name="spread", bufs=IN_FLIGHT)
+                nc.scalar.copy(out=spread[k][:], in_=spread_psum[k][:])
 
-        def turn(pr):
-            turn_pe(pr)
-            turn_s(pr)
+        def quantise_e(k):
+            e_words[k] = work.tile([P, CHUNK], U32, name="e_words", bufs=IN_FLIGHT, align_bytes=64)
+            e_scales[k] = work.tile([P, CHUNK], U8, name="e_scales", bufs=IN_FLIGHT, align_bytes=64)
+            nc.vector.quantize_mx(
+                out=e_words[k][:].bitcast(FP8X4), scales=e_scales[k][:], in_=e_grouped[k][:].rearrange("p n t -> p (n t)")
+            )
 
-        def back(u):
-            k, j = divmod(u, 4)
+        def product(number):
+            k, j = divmod(number, 4)
             b = k // 4
-            cols = slice((k % 4) * 512, (k % 4) * 512 + 512)
+            pixels = slice((k % 4) * CHUNK, (k % 4 + 1) * CHUNK)
             if j == 0:
-                y_t[k] = work.tile([P, 4, 512], F32, name="y", tag="big", bufs=3, align_bytes=64)
-            num = bank(3 + u % 2, [P, 512], F32, "num")
+                result[k] = work.tile([P, PACK, CHUNK], F32, name="result", bufs=IN_FLIGHT)
+            summed = psum_bank(PRODUCT_BANKS[number % 2], [P, CHUNK], F32, "summed")
             nc.tensor.matmul_mx(
-                out=num[:],
-                lhsT=c3q[b][:, j * P : j * P + P].bitcast(FP8X4),
-                lhsT_scale=c3s[b][:, j * P : j * P + P],
-                rhs=eq_t[k][:].bitcast(FP8X4),
-                rhs_scale=es_t[k][:],
+                out=summed[:],
+                lhsT=c3p_words[b][:, j * P : (j + 1) * P].bitcast(FP8X4),
+                lhsT_scale=c3p_scales[b][:, j * P : (j + 1) * P],
+                rhs=e_words[k][:].bitcast(FP8X4),
+                rhs_scale=e_scales[k][:],
                 start=True,
                 stop=True,
             )
             nc.vector.scalar_tensor_tensor(
-                out=y_t[k][:, j, :], in0=num[:], scalar=gam[:, 0:1], in1=r_t[k][:], op0=ALU.mult, op1=ALU.mult
+                out=result[k][:, j, :],
+                in0=summed[:],
+                scalar=gamma_f32[:, 0:1],
+                in1=spread[k][:],
+                op0=ALU.mult,
+                op1=ALU.mult,
             )
-            adder = nc.vector if ((u >= TICKS - TAIL_V and u % 2 == 1) or (u % ADP in ADV)) else nc.gpsimd
+            adder = nc.vector if (number >= TILES - SHARED_ADDS and number % 2 == 1) else nc.gpsimd
             adder.tensor_tensor(
-                out=y_t[k][:, j, :], in0=y_t[k][:, j, :], in1=x_sb[k // 2][:, j, (k % 2) * 512 : (k % 2) * 512 + 512],
+                out=result[k][:, j, :],
+                in0=result[k][:, j, :],
+                in1=x_sb[k // 2][:, j, (k % 2) * CHUNK : (k % 2 + 1) * CHUNK],
                 op=ALU.add,
             )
             if k == CHUNKS - 1:
-                nc.sync.dma_start(out=out_v[b][:, j, cols], in_=y_t[k][:, j, :])
+                nc.sync.dma_start(out=out_view[b][:, j, pixels], in_=result[k][:, j, :])
             elif j == 3:
-                nc.sync.dma_start(out=out_v[b][:, :, cols], in_=y_t[k][:])
+                nc.sync.dma_start(out=out_view[b][:, :, pixels], in_=result[k][:])
 
-        done = set()
-
-        def due(kind, t, lag, step, count):
-            idx, rem = divmod(t - lag, step)
-            if t < lag or rem != 0 or idx >= count or (kind, idx) in done:
-                return None
-            done.add((kind, idx))
-            return idx
-
-        def tick(t, fronts, with_back):
-            k = due("rc", t, LAG_RC, 4, fronts // 4)
-            if k is not None:
-                recip(k)
-            if t < fronts and ("f", t) not in done:
-                done.add(("f", t))
-                front(t)
-            if QPOS == 0:
-                k = due("q", t, LAG_Q, 4, fronts // 4)
-                if k is not None:
-                    quantise_e(k)
-            if with_back and LAG_MX <= t < TICKS + LAG_MX:
-                back(t - LAG_MX)
-            if QPOS == 1:
-                k = due("q", t, LAG_Q, 4, fronts // 4)
-                if k is not None:
-                    quantise_e(k)
-            pr = due("te", t, LAG_TE, 2, fronts // 2)
-            if pr is not None:
-                turn(pr)
-
-        for t in range(HEAD):
-            done.add(("f", t))
-            front(t)
-            for act in HEAD_PLAN.get(t, ()):
-                if act[0] == "w3":
-                    prepare_w3()
-                elif act[0] == "qw3":
-                    quantise_w3()
-                elif act[0] == "qx":
-                    quantise_x(0)
-                else:
-                    regroup_x(act[1], {act[2]: act[3]}, (act[2],))
-        for k in range(HEAD // 4):
-            done.add(("rc", k))
-            done.add(("q", k))
-            done.add(("te", 2 * k))
-            done.add(("te", 2 * k + 1))
-        vector_extras = {0: [(recip, 0)], 2: [(quantise_e, 0), (recip, 1)], 4: [(quantise_e, 1)]}
-        for g in range(NHALF):
-            pool_half(g, vector_extras.get(g, []), g if g < HEAD // 2 else None)
-        nc.vector.tensor_copy(out=gam[:], in_=gam_bf[:])
-        for t in range(HEAD, TICKS + LAG_MX):
-            tick(t, TICKS, True)
-            if t == HEAD + 3:
+        for t in range(EARLY_TILES):
+            scores_and_exponentials(t)
+            if t == 2:
+                transpose_w3()
+                quantise_w3()
+            if t == 3:
+                regroup_x(0, REGROUP_HALF_0)
+            if t == 5:
+                quantise_x(0)
+                regroup_x(1, REGROUP_HALF_1)
+        for g in range(HALVES):
+            pool_half(g)
+        nc.vector.tensor_copy(out=gamma_f32[:], in_=gamma_bf[:])
+        for step in range(EARLY_TILES, TILES + PRODUCT_LAG):
+            k, rest = divmod(step - RECIPROCAL_LAG, 4)
+            if rest == 0 and EARLY_CHUNKS <= k < CHUNKS:
+                reciprocal_of_sums(k)
+            if step < TILES:
+                scores_and_exponentials(step)
+            if step >= PRODUCT_LAG:
+                product(step - PRODUCT_LAG)
+            k, rest = divmod(step - QUANTISE_LAG, 4)
+            if rest == 0 and EARLY_CHUNKS <= k < CHUNKS:
+                quantise_e(k)
+            pair, rest = divmod(step - TURN_LAG, 2)
+            if rest == 0 and EARLY_TILES // 2 <= pair < TILES // 2:
+                transpose_pair(pair)
+                copy_pair(pair)
+            if step == EARLY_TILES + 3:
                 quantise_c3p(B - 1)

@@ -45,10 +45,18 @@ PRODUCT_BANKS = (3, 4)
 TURN_BANKS = (5, 6)
 SPREAD_BANK = 7
 
-REGROUP_HALF_0 = "vvgg"
-REGROUP_HALF_1 = "vsvs"
 REGROUP_BESIDE_TURNS = "ssgg"
 REGROUP_LATER = "sssg"
+FIRST_REGROUPS = (
+    (2, 0, 3, "g"),
+    (4, 0, 1, "v"),
+    (5, 0, 2, "g"),
+    (5, 1, 1, "s"),
+    (6, 0, 0, "v"),
+    (7, 1, 0, "v"),
+    (8, 1, 2, "v"),
+    (8, 1, 3, "s"),
+)
 
 
 def tile_selfspatialattentionmodule_pb_t_kernel(tc, x, c2, c1p, W3, gamma, out):
@@ -137,17 +145,18 @@ def tile_selfspatialattentionmodule_pb_t_kernel(tc, x, c2, c1p, W3, gamma, out):
         x_words = {}
         x_scales = {}
 
-        def regroup_x(g, engines):
-            x_grouped[g] = work.tile([P, 4, POOLED, PACK], BF16, name="x_grouped", align_bytes=64)
+        def regroup_piece(g, piece, engine):
+            if g not in x_grouped:
+                x_grouped[g] = work.tile([P, 4, POOLED, PACK], BF16, name="x_grouped", align_bytes=64)
             src = x_sb[g][:].rearrange("p j (i dh jj dw) -> p dh i jj dw j", i=16, dh=2, jj=16, dw=2)
-            for piece in range(4):
-                dh, rows = divmod(piece, 2)
-                dst = x_grouped[g][:, 2 * dh : 2 * dh + 2, P * rows : P * (rows + 1), :]
-                copy_on(
-                    engines[piece],
-                    dst.rearrange("p dw (i jj) j -> p i jj dw j", i=8),
-                    src[:, dh, 8 * rows : 8 * (rows + 1)],
-                )
+            dh, rows = divmod(piece, 2)
+            dst = x_grouped[g][:, 2 * dh : 2 * dh + 2, P * rows : P * (rows + 1), :]
+            copy_on(engine, dst.rearrange("p dw (i jj) j -> p i jj dw j", i=8), src[:, dh, 8 * rows : 8 * (rows + 1)])
+
+        def first_regroups(tile_no):
+            for behind, g, piece, engine in FIRST_REGROUPS:
+                if behind == tile_no:
+                    regroup_piece(g, piece, engine)
 
         def quantise_x(g):
             x_words[g] = work.tile([P, 4 * POOLED], U32, name="x_words", align_bytes=64)
@@ -203,6 +212,8 @@ def tile_selfspatialattentionmodule_pb_t_kernel(tc, x, c2, c1p, W3, gamma, out):
                         nc.vector.tensor_tensor(out=largest[part][:], in0=largest[part][:], in1=c3[:], op=ALU.max)
                 if member == 0 and early_pair is not None:
                     copy_pair(early_pair)
+                if member == 0 and g == 0:
+                    first_regroups(EARLY_TILES)
             if g + 1 < HALVES:
                 quantise_x(g + 1)
             if not second and b > 0:
@@ -224,7 +235,9 @@ def tile_selfspatialattentionmodule_pb_t_kernel(tc, x, c2, c1p, W3, gamma, out):
                     op1=ALU.add,
                 )
             if g + 2 < HALVES:
-                regroup_x(g + 2, REGROUP_BESIDE_TURNS if early_pair is not None else REGROUP_LATER)
+                engines = REGROUP_BESIDE_TURNS if early_pair is not None else REGROUP_LATER
+                for piece in range(4):
+                    regroup_piece(g + 2, piece, engines[piece])
             if second:
                 c3p_grouped[b] = work.tile([P, C, PACK], BF16, name="c3p_grouped", tag="grouped", bufs=2, align_bytes=64)
                 copy_on("g", c3p_grouped[b][:], c3p_planes[b][:].rearrange("p t c -> p c t"))
@@ -353,11 +366,9 @@ def tile_selfspatialattentionmodule_pb_t_kernel(tc, x, c2, c1p, W3, gamma, out):
             if t == 2:
                 transpose_w3()
                 quantise_w3()
-            if t == 3:
-                regroup_x(0, REGROUP_HALF_0)
-            if t == 5:
+            first_regroups(t)
+            if t == 6:
                 quantise_x(0)
-                regroup_x(1, REGROUP_HALF_1)
         for g in range(HALVES):
             pool_half(g)
         nc.vector.tensor_copy(out=gamma_f32[:], in_=gamma_bf[:])

@@ -26,37 +26,19 @@ POOLED = HALF // 4
 CHUNK = 4 * P
 TILES = B * N // P
 CHUNKS = TILES // 4
-EARLY_CHUNKS = 2
-EARLY_TILES = 4 * EARLY_CHUNKS
-
-TURN_LAG = 3
-RECIPROCAL_LAG = 5
-QUANTISE_LAG = 7
-PRODUCT_LAG = 9
-SHARED_ADDS = 8
+PRODUCT_LAG = 2
+PERIODS = CHUNKS + PRODUCT_LAG
+TAIL_VECTOR = (2, 3)
 IN_FLIGHT = 3
 
-W3_BANKS = (3, 4)
-C3_BANKS = (0, 1, 2, 3)
-EARLY_TURN_BANKS = (4, 5)
-SUM_BANKS = (6, 7)
 SCORE_BANKS = (0, 1, 2)
-PRODUCT_BANKS = (3, 4)
+C3_BANKS = (3, 4)
 TURN_BANKS = (5, 6)
-SPREAD_BANK = 7
+ROWS_BANK = 7
+PRODUCT_BANKS = (6, 7)
 
-REGROUP_BESIDE_TURNS = "ssgg"
+REGROUP_FIRST = ("vvgs", "sgsv")
 REGROUP_LATER = "sssg"
-FIRST_REGROUPS = (
-    (2, 0, 3, "g"),
-    (4, 0, 1, "v"),
-    (5, 0, 2, "g"),
-    (5, 1, 1, "s"),
-    (6, 0, 0, "v"),
-    (7, 1, 0, "v"),
-    (8, 1, 2, "v"),
-    (8, 1, 3, "s"),
-)
 
 
 def tile_selfspatialattentionmodule_pb_t_kernel(tc, x, c2, c1p, W3, gamma, out):
@@ -65,6 +47,7 @@ def tile_selfspatialattentionmodule_pb_t_kernel(tc, x, c2, c1p, W3, gamma, out):
         keep = ctx.enter_context(tc.tile_pool(name="keep", bufs=1))
         work = ctx.enter_context(tc.tile_pool(name="work", bufs=2))
         psum = ctx.enter_context(tc.psum_pool(name="psum", bufs=1))
+        ctx.enter_context(tc.manual_schedule())
 
         def psum_bank(index, shape, dtype, name):
             return psum.tile(shape, dtype, name=name, tag="bank%d" % index)
@@ -78,9 +61,12 @@ def tile_selfspatialattentionmodule_pb_t_kernel(tc, x, c2, c1p, W3, gamma, out):
         def pixels_of_half(g):
             return slice((g % 2) * HALF, (g % 2 + 1) * HALF)
 
-        def load_x(g):
+        def load_x(g, pieces=1):
             view = x[g // 2].rearrange("(p j) h w -> p j (h w)", j=PACK)
-            nc.sync.dma_start(out=x_sb[g][:], in_=view[:, :, pixels_of_half(g)])
+            width = HALF // pieces
+            for first in range(0, HALF, width):
+                start = (g % 2) * HALF + first
+                nc.sync.dma_start(out=x_sb[g][:, :, first : first + width], in_=view[:, :, start : start + width])
 
         def load_c2(g):
             view = c2[g // 2].rearrange("(u p) h w -> p u (h w)", u=2)
@@ -92,14 +78,15 @@ def tile_selfspatialattentionmodule_pb_t_kernel(tc, x, c2, c1p, W3, gamma, out):
         load_c1(0)
         load_c2(0)
         nc.sync.dma_start(out=w3_sb[:], in_=W3.rearrange("(p a) i -> p a i", a=PACK))
-        for g in range(HALVES):
-            load_x(g)
+        load_x(0, 2)
+        load_x(1)
         nc.sync.dma_start(out=gamma_bf[:], in_=gamma.partition_broadcast(P))
         load_c2(1)
-        for b in range(1, B):
-            load_c1(b)
-            load_c2(2 * b)
-            load_c2(2 * b + 1)
+        for g in range(2, HALVES):
+            load_x(g)
+            if g % 2 == 0:
+                load_c1(g // 2)
+            load_c2(g)
 
         ident_bf = keep.tile([P, P], BF16, name="ident_bf")
         make_identity(nc, ident_bf[:])
@@ -110,6 +97,9 @@ def tile_selfspatialattentionmodule_pb_t_kernel(tc, x, c2, c1p, W3, gamma, out):
         nc.vector.memset(warm_in[:], 0.0)
         nc.scalar.activation(out=warm_out[:], in_=warm_in[:], func=ACT.Exp)
         gamma_f32 = keep.tile([P, 1], F32, name="gamma_f32")
+        reciprocals = [keep.tile([P, P], F32, name="reciprocals%d" % i) for i in range(2)]
+        for i in range(2):
+            nc.gpsimd.memset(reciprocals[i][:], 0.0)
 
         def copy_on(engine, dst, src):
             if engine == "v":
@@ -123,18 +113,22 @@ def tile_selfspatialattentionmodule_pb_t_kernel(tc, x, c2, c1p, W3, gamma, out):
         w3_words = keep.tile([P, C], U32, name="w3_words", align_bytes=64)
         w3_scales = keep.tile([P, C], U8, name="w3_scales", align_bytes=64)
 
+        turned_w3 = {}
+
         def transpose_w3():
             pairs = w3_sb[:].bitcast(F32).rearrange("p a (q u) -> p a u q", u=2)
-            grouped_pairs = w3_grouped[:].bitcast(F32)
             for h in range(2):
-                turned = psum_bank(W3_BANKS[h], [P, 2, 2, P], F32, "w3_turned")
+                turned_w3[h] = psum_bank(PRODUCT_BANKS[h], [P, 2, 2, P], F32, "turned_w3")
                 for u in range(2):
                     for a in range(2):
-                        nc.tensor.transpose(turned[:, u, a, :], pairs[:, 2 * h + a, u, :], ident_f32[:])
-                nc.vector.tensor_copy(
-                    out=grouped_pairs[:, 2 * P * h : 2 * P * (h + 1), :].rearrange("p (a q) u -> p a q u", a=2),
-                    in_=turned[:].rearrange("p u a q -> p a q u"),
-                )
+                        nc.tensor.transpose(turned_w3[h][:, u, a, :], pairs[:, 2 * h + a, u, :], ident_f32[:])
+
+        def copy_w3(h, engine):
+            copy_on(
+                engine,
+                w3_grouped[:].bitcast(F32)[:, 2 * P * h : 2 * P * (h + 1), :].rearrange("p (a q) u -> p a q u", a=2),
+                turned_w3[h][:].rearrange("p u a q -> p a q u"),
+            )
 
         def quantise_w3():
             nc.vector.quantize_mx(
@@ -145,45 +139,74 @@ def tile_selfspatialattentionmodule_pb_t_kernel(tc, x, c2, c1p, W3, gamma, out):
         x_words = {}
         x_scales = {}
 
-        def regroup_piece(g, piece, engine):
-            if g not in x_grouped:
-                x_grouped[g] = work.tile([P, 4, POOLED, PACK], BF16, name="x_grouped", align_bytes=64)
+        def regroup_piece(part, dh, engine):
+            if part not in x_grouped:
+                x_grouped[part] = work.tile([P, 4, P, PACK], BF16, name="x_grouped", bufs=3, align_bytes=64)
+            g, rows = divmod(part, 2)
             src = x_sb[g][:].rearrange("p j (i dh jj dw) -> p dh i jj dw j", i=16, dh=2, jj=16, dw=2)
-            dh, rows = divmod(piece, 2)
-            dst = x_grouped[g][:, 2 * dh : 2 * dh + 2, P * rows : P * (rows + 1), :]
+            dst = x_grouped[part][:, 2 * dh : 2 * dh + 2, :, :]
             copy_on(engine, dst.rearrange("p dw (i jj) j -> p i jj dw j", i=8), src[:, dh, 8 * rows : 8 * (rows + 1)])
 
-        def first_regroups(tile_no):
-            for behind, g, piece, engine in FIRST_REGROUPS:
-                if behind == tile_no:
-                    regroup_piece(g, piece, engine)
-
-        def quantise_x(g):
-            x_words[g] = work.tile([P, 4 * POOLED], U32, name="x_words", align_bytes=64)
-            x_scales[g] = work.tile([P, 4 * POOLED], U8, name="x_scales", align_bytes=64)
+        def quantise_x(part):
+            x_words[part] = work.tile([P, 4 * P], U32, name="x_words", bufs=3, align_bytes=64)
+            x_scales[part] = work.tile([P, 4 * P], U8, name="x_scales", bufs=3, align_bytes=64)
             nc.vector.quantize_mx(
-                out=x_words[g][:].bitcast(FP8X4),
-                scales=x_scales[g][:],
-                in_=x_grouped[g][:].rearrange("p m q j -> p (m q j)"),
+                out=x_words[part][:].bitcast(FP8X4),
+                scales=x_scales[part][:],
+                in_=x_grouped[part][:].rearrange("p m q j -> p (m q j)"),
             )
 
         c3p_words = [keep.tile([P, C], U32, name="c3p_words%d" % b, align_bytes=64) for b in range(B)]
         c3p_scales = [keep.tile([P, C], U8, name="c3p_scales%d" % b, align_bytes=64) for b in range(B)]
         c3p_planes = {}
         c3p_grouped = {}
-        c3_count = [0]
+        c3 = {}
+        largest = {}
 
-        def step_1_pass(dst, g, member, part, start, stop):
-            cols = slice(member * POOLED + part * P, member * POOLED + (part + 1) * P)
+        def step_1_pass(dst, part, member, start, stop):
+            cols = slice(member * P, (member + 1) * P)
             nc.tensor.matmul_mx(
                 out=dst[:],
-                lhsT=x_words[g][:, cols].bitcast(FP8X4),
-                lhsT_scale=x_scales[g][:, cols],
+                lhsT=x_words[part][:, cols].bitcast(FP8X4),
+                lhsT_scale=x_scales[part][:, cols],
                 rhs=w3_words[:].bitcast(FP8X4),
                 rhs_scale=w3_scales[:],
                 start=start,
                 stop=stop,
             )
+
+        def make_c3(part, member, bank):
+            c3[part, member] = psum_bank(bank, [P, C], F32, "c3")
+            members = range(4) if member == 4 else [member]
+            for m in members:
+                step_1_pass(c3[part, member], part, m, m == members[0], m == members[-1])
+
+        def use_c3(part, member):
+            read = c3[part, member]
+            if member == 0:
+                largest[part] = work.tile([P, C], F32, name="largest", bufs=3)
+                nc.scalar.copy(out=largest[part][:], in_=read[:])
+            elif member < 4:
+                nc.vector.tensor_tensor(out=largest[part][:], in0=largest[part][:], in1=read[:], op=ALU.max)
+            else:
+                b, plane = divmod(part, 4)
+                if plane == 0:
+                    c3p_planes[b] = work.tile([P, PACK, C], BF16, name="c3p_planes")
+                nc.vector.scalar_tensor_tensor(
+                    out=c3p_planes[b][:, plane, :],
+                    in0=read[:],
+                    scalar=0.25,
+                    in1=largest[part][:],
+                    op0=ALU.mult,
+                    op1=ALU.add,
+                )
+
+        def group_c3p(b, quarters, engine):
+            if b not in c3p_grouped:
+                c3p_grouped[b] = work.tile([P, C, PACK], BF16, name="c3p_grouped", bufs=1, align_bytes=64)
+            for quarter in quarters:
+                channels = slice(quarter * P, (quarter + 1) * P)
+                copy_on(engine, c3p_grouped[b][:, channels, :], c3p_planes[b][:, :, channels].rearrange("p t c -> p c t"))
 
         def quantise_c3p(b):
             nc.vector.quantize_mx(
@@ -192,91 +215,45 @@ def tile_selfspatialattentionmodule_pb_t_kernel(tc, x, c2, c1p, W3, gamma, out):
                 in_=c3p_grouped[b][:].rearrange("p c t -> p (c t)"),
             )
 
-        def pool_half(g):
-            b, second = divmod(g, 2)
-            early_pair = g if g < EARLY_TILES // 2 else None
-            if early_pair is not None:
-                transpose_pair(early_pair)
-            if not second:
-                c3p_planes[b] = work.tile([P, PACK, C], BF16, name="c3p_planes", tag="four_planes", bufs=IN_FLIGHT)
-            largest = {}
-            for member in range(4):
-                for part in range(2):
-                    c3 = psum_bank(C3_BANKS[c3_count[0] % len(C3_BANKS)], [P, C], F32, "c3")
-                    c3_count[0] += 1
-                    step_1_pass(c3, g, member, part, True, True)
-                    if member == 0:
-                        largest[part] = work.tile([P, C], F32, name="largest%d" % part)
-                        nc.scalar.copy(out=largest[part][:], in_=c3[:])
-                    else:
-                        nc.vector.tensor_tensor(out=largest[part][:], in0=largest[part][:], in1=c3[:], op=ALU.max)
-                if member == 0 and early_pair is not None:
-                    copy_pair(early_pair)
-                if member == 0 and g == 0:
-                    first_regroups(EARLY_TILES)
-            if g + 1 < HALVES:
-                quantise_x(g + 1)
-            if not second and b > 0:
-                quantise_c3p(b - 1)
-            if not second and 0 < b <= EARLY_CHUNKS:
-                quantise_e(b - 1)
-            if not second and b < EARLY_CHUNKS:
-                reciprocal_of_sums(b)
-            for part in range(2):
-                total = psum_bank(SUM_BANKS[part], [P, C], F32, "total")
-                for member in range(4):
-                    step_1_pass(total, g, member, part, member == 0, member == 3)
-                nc.vector.scalar_tensor_tensor(
-                    out=c3p_planes[b][:, 2 * second + part, :],
-                    in0=total[:],
-                    scalar=0.25,
-                    in1=largest[part][:],
-                    op0=ALU.mult,
-                    op1=ALU.add,
-                )
-            if g + 2 < HALVES:
-                engines = REGROUP_BESIDE_TURNS if early_pair is not None else REGROUP_LATER
-                for piece in range(4):
-                    regroup_piece(g + 2, piece, engines[piece])
-            if second:
-                c3p_grouped[b] = work.tile([P, C, PACK], BF16, name="c3p_grouped", tag="grouped", bufs=2, align_bytes=64)
-                copy_on("g", c3p_grouped[b][:], c3p_planes[b][:].rearrange("p t c -> p c t"))
-
+        scores = {}
         negative_max = {}
         sums = {}
         e_bf = {}
-        e_turned = {}
+        turned = {}
+        rows_psum = {}
         e_grouped = {}
         e_words = {}
         e_scales = {}
-        reciprocals = {}
-        spread_psum = {}
         spread = {}
+        summed = {}
         result = {}
         out_view = [out[b].rearrange("(p j) h w -> p j (h w)", j=PACK) for b in range(B)]
 
-        def scores_and_exponentials(t):
+        def make_scores(t):
             k, i = divmod(t, 4)
             first = (k % 2) * CHUNK + i * P
-            if i == 0:
-                negative_max[k] = work.tile([P, 4], F32, name="negative_max", bufs=IN_FLIGHT)
-                sums[k] = work.tile([P, 4], F32, name="sums", bufs=IN_FLIGHT)
-                e_bf[k] = work.tile([P, 4, M], BF16, name="e_bf", tag="four_planes", bufs=IN_FLIGHT)
-            scores = psum_bank(SCORE_BANKS[t % len(SCORE_BANKS)], [P, M], F32, "scores")
+            scores[t] = psum_bank(SCORE_BANKS[t % len(SCORE_BANKS)], [P, M], F32, "scores")
             for u in range(2):
                 nc.tensor.matmul(
-                    out=scores[:],
+                    out=scores[t][:],
                     lhsT=c2_sb[k // 2][:, u, first : first + P],
                     rhs=c1_sb[k // 4][:, u, :],
                     start=u == 0,
                     stop=u == 1,
                 )
+
+        def use_scores(t):
+            k, i = divmod(t, 4)
+            if i == 0:
+                negative_max[k] = work.tile([P, 4], F32, name="negative_max", bufs=IN_FLIGHT)
+                sums[k] = work.tile([P, 4], F32, name="sums", bufs=IN_FLIGHT)
+                e_bf[k] = work.tile([P, 4, M], BF16, name="e_bf", bufs=IN_FLIGHT)
             nc.vector.tensor_reduce(
-                out=negative_max[k][:, i : i + 1], in_=scores[:], axis=AX.X, op=ALU.max, negate=True
+                out=negative_max[k][:, i : i + 1], in_=scores[t][:], axis=AX.X, op=ALU.max, negate=True
             )
             nc.scalar.activation(
                 out=e_bf[k][:, i, :],
-                in_=scores[:],
+                in_=scores[t][:],
                 func=ACT.Exp,
                 bias=negative_max[k][:, i : i + 1],
                 scale=1.0,
@@ -284,39 +261,44 @@ def tile_selfspatialattentionmodule_pb_t_kernel(tc, x, c2, c1p, W3, gamma, out):
             )
 
         def reciprocal_of_sums(k):
-            reciprocals[k] = work.tile([P, 4], F32, name="reciprocals")
-            nc.vector.reciprocal(out=reciprocals[k][:], in_=sums[k][:])
+            nc.vector.reciprocal(out=reciprocals[k % 2][:, 0:4], in_=sums[k][:])
 
-        def transpose_pair(pair):
-            k, second = divmod(pair, 2)
-            early = pair < EARLY_TILES // 2
-            banks = EARLY_TURN_BANKS if early else TURN_BANKS
-            e_turned[pair] = psum_bank(banks[pair % 2], [P, 2, PACK, P], BF16, "e_turned")
+        def transpose_pair(k, second):
+            turned[second] = psum_bank(TURN_BANKS[second], [P, 2, PACK, P], BF16, "turned")
             for i in range(2):
                 for t in range(PACK):
                     nc.tensor.transpose(
-                        e_turned[pair][:, i, t, :], e_bf[k][:, 2 * second + i, t * P : (t + 1) * P], ident_bf[:]
-                    )
-            if second:
-                spread_psum[k] = psum_bank(EARLY_TURN_BANKS[0] if early else SPREAD_BANK, [P, CHUNK], F32, "spread_psum")
-                for i in range(4):
-                    nc.tensor.transpose(
-                        spread_psum[k][:, i * P : (i + 1) * P],
-                        reciprocals[k][:, i : i + 1].to_broadcast([P, P]),
-                        ident_f32[:],
+                        turned[second][:, i, t, :], e_bf[k][:, 2 * second + i, t * P : (t + 1) * P], ident_bf[:]
                     )
 
-        def copy_pair(pair):
-            k, second = divmod(pair, 2)
-            if not second:
-                e_grouped[k] = work.tile([P, CHUNK, PACK], BF16, name="e_grouped", tag="grouped", bufs=2, align_bytes=64)
+        def transpose_rows(k):
+            rows_psum[0] = psum_bank(ROWS_BANK, [P, P], F32, "rows_psum")
+            nc.tensor.transpose(rows_psum[0][:], reciprocals[k % 2][:], ident_f32[:])
+
+        def copy_pair(k, second):
+            if k not in e_grouped:
+                e_grouped[k] = work.tile([P, CHUNK, PACK], BF16, name="e_grouped", align_bytes=64)
             nc.scalar.copy(
                 out=e_grouped[k][:, 2 * P * second : 2 * P * (second + 1), :].rearrange("p (i n) t -> p i n t", i=2),
-                in_=e_turned[pair][:].rearrange("p i t n -> p i n t"),
+                in_=turned[second][:].rearrange("p i t n -> p i n t"),
             )
-            if second:
-                spread[k] = work.tile([P, CHUNK], F32, name="spread", bufs=IN_FLIGHT)
-                nc.scalar.copy(out=spread[k][:], in_=spread_psum[k][:])
+
+        def spread_on_chip(k):
+            banks = psum_bank(ROWS_BANK, [P, CHUNK], F32, "spread_psum")
+            for i in range(4):
+                nc.tensor.transpose(
+                    banks[:, i * P : (i + 1) * P], reciprocals[k % 2][:, i : i + 1].to_broadcast([P, P]), ident_f32[:]
+                )
+            spread[k] = work.tile([P, CHUNK], F32, name="spread", bufs=IN_FLIGHT)
+            nc.scalar.copy(out=spread[k][:], in_=banks[:])
+
+        def spread_rows(k):
+            spread[k] = work.tile([P, CHUNK], F32, name="spread", bufs=IN_FLIGHT)
+            rows = work.tile([P, P], F32, name="rows")
+            nc.scalar.copy(out=rows[:], in_=rows_psum[0][:])
+            parked = out[B - 1, k, H - CHUNK // W : H, :]
+            nc.sync.dma_start(out=parked.rearrange("(i h) w -> i (h w)", i=4), in_=rows[0:4, :])
+            nc.sync.dma_start(out=spread[k][:], in_=parked.rearrange("h w -> (h w)").partition_broadcast(P))
 
         def quantise_e(k):
             e_words[k] = work.tile([P, CHUNK], U32, name="e_words", bufs=IN_FLIGHT, align_bytes=64)
@@ -325,15 +307,11 @@ def tile_selfspatialattentionmodule_pb_t_kernel(tc, x, c2, c1p, W3, gamma, out):
                 out=e_words[k][:].bitcast(FP8X4), scales=e_scales[k][:], in_=e_grouped[k][:].rearrange("p n t -> p (n t)")
             )
 
-        def product(number):
-            k, j = divmod(number, 4)
+        def make_product(k, j, banks=PRODUCT_BANKS):
             b = k // 4
-            pixels = slice((k % 4) * CHUNK, (k % 4 + 1) * CHUNK)
-            if j == 0:
-                result[k] = work.tile([P, PACK, CHUNK], F32, name="result", bufs=IN_FLIGHT)
-            summed = psum_bank(PRODUCT_BANKS[number % 2], [P, CHUNK], F32, "summed")
+            summed[k, j] = psum_bank(banks[(j + 1) % 2], [P, CHUNK], F32, "summed")
             nc.tensor.matmul_mx(
-                out=summed[:],
+                out=summed[k, j][:],
                 lhsT=c3p_words[b][:, j * P : (j + 1) * P].bitcast(FP8X4),
                 lhsT_scale=c3p_scales[b][:, j * P : (j + 1) * P],
                 rhs=e_words[k][:].bitcast(FP8X4),
@@ -341,51 +319,237 @@ def tile_selfspatialattentionmodule_pb_t_kernel(tc, x, c2, c1p, W3, gamma, out):
                 start=True,
                 stop=True,
             )
+
+        def use_product(k, j):
+            if j == 0:
+                result[k] = work.tile([P, PACK, CHUNK], F32, name="result", bufs=IN_FLIGHT)
             nc.vector.scalar_tensor_tensor(
                 out=result[k][:, j, :],
-                in0=summed[:],
+                in0=summed[k, j][:],
                 scalar=gamma_f32[:, 0:1],
                 in1=spread[k][:],
                 op0=ALU.mult,
                 op1=ALU.mult,
             )
-            adder = nc.vector if (number >= TILES - SHARED_ADDS and number % 2 == 1) else nc.gpsimd
-            adder.tensor_tensor(
+            if k < 12 or j not in TAIL_VECTOR:
+                add_x(k, j, nc.gpsimd)
+
+        def add_x(k, j, engine):
+            engine.tensor_tensor(
                 out=result[k][:, j, :],
                 in0=result[k][:, j, :],
                 in1=x_sb[k // 2][:, j, (k % 2) * CHUNK : (k % 2 + 1) * CHUNK],
                 op=ALU.add,
             )
-            if k == CHUNKS - 1:
-                nc.sync.dma_start(out=out_view[b][:, j, pixels], in_=result[k][:, j, :])
-            elif j == 3:
-                nc.sync.dma_start(out=out_view[b][:, :, pixels], in_=result[k][:])
 
-        for t in range(EARLY_TILES):
-            scores_and_exponentials(t)
-            if t == 2:
-                transpose_w3()
-                quantise_w3()
-            first_regroups(t)
-            if t == 6:
-                quantise_x(0)
-        for g in range(HALVES):
-            pool_half(g)
+        def store(k, j=None):
+            b = k // 4
+            pixels = slice((k % 4) * CHUNK, (k % 4 + 1) * CHUNK)
+            if j is None:
+                nc.sync.dma_start(out=out_view[b][:, :, pixels], in_=result[k][:])
+            else:
+                nc.sync.dma_start(out=out_view[b][:, j, pixels], in_=result[k][:, j, :])
+
+        def scores_of(c, i):
+            if c < CHUNKS:
+                make_scores(4 * c + i)
+
+        def exps_of(c, i):
+            if c < CHUNKS:
+                use_scores(4 * c + i)
+
+        bank_count = [0]
+
+        def ring5(part, member):
+            make_c3(part, member, 3 + bank_count[0] % 5)
+            bank_count[0] += 1
+
+        def transposes(k):
+            reciprocal_of_sums(k)
+            transpose_pair(k, 0)
+            transpose_pair(k, 1)
+            if k < CHUNKS - 1:
+                transpose_rows(k)
+                spread_rows(k)
+            else:
+                spread_on_chip(k)
+            copy_pair(k, 1)
+            copy_pair(k, 0)
+
+        scores_of(0, 0)
+        scores_of(0, 1)
+        transpose_w3()
+        scores_of(0, 2)
+        exps_of(0, 0)
+        copy_w3(0, "s")
+        copy_w3(1, "s")
+        exps_of(0, 1)
+        scores_of(0, 3)
+        regroup_piece(0, 0, "v")
+        regroup_piece(0, 1, "v")
+        regroup_piece(1, 0, "s")
+        exps_of(0, 2)
+        quantise_w3()
+        quantise_x(0)
+        for member in range(3):
+            ring5(0, member)
+        use_c3(0, 0)
+        regroup_piece(1, 1, "s")
+        exps_of(0, 3)
+        scores_of(1, 0)
+        ring5(0, 3)
+        ring5(0, 4)
+        regroup_piece(2, 0, "g")
+        regroup_piece(2, 1, "g")
+        scores_of(1, 1)
+        use_c3(0, 1)
+        exps_of(1, 0)
+        use_c3(0, 2)
+        quantise_x(1)
+        use_c3(0, 3)
+        for member in range(3):
+            ring5(1, member)
+        use_c3(1, 0)
+        exps_of(1, 1)
+        scores_of(1, 2)
+        use_c3(0, 4)
+        use_c3(1, 1)
+        ring5(1, 3)
+        ring5(1, 4)
+        quantise_x(2)
+        regroup_piece(3, 0, "g")
+        regroup_piece(3, 1, "s")
+        for member in range(3):
+            ring5(2, member)
+        use_c3(2, 0)
+        use_c3(1, 2)
+        exps_of(1, 2)
+        scores_of(1, 3)
+        use_c3(1, 3)
+        use_c3(2, 1)
+        ring5(2, 3)
+        ring5(2, 4)
+        regroup_piece(4, 0, "s")
+        use_c3(1, 4)
+        quantise_x(3)
+        use_c3(2, 2)
+        scores_of(2, 0)
+        for member in range(3):
+            ring5(3, member)
+        use_c3(3, 0)
+        exps_of(1, 3)
+        regroup_piece(4, 1, "g")
+        use_c3(2, 3)
+        use_c3(3, 1)
+        ring5(3, 3)
+        ring5(3, 4)
+        use_c3(2, 4)
+        use_c3(3, 2)
+        scores_of(2, 1)
+        quantise_x(4)
+        make_c3(4, 0, 3)
+        use_c3(3, 3)
+        transposes(0)
+        make_c3(4, 1, 4)
+        use_c3(3, 4)
+        group_c3p(0, range(4), "g")
+        scores_of(2, 2)
         nc.vector.tensor_copy(out=gamma_f32[:], in_=gamma_bf[:])
-        for step in range(EARLY_TILES, TILES + PRODUCT_LAG):
-            k, rest = divmod(step - RECIPROCAL_LAG, 4)
-            if rest == 0 and EARLY_CHUNKS <= k < CHUNKS:
-                reciprocal_of_sums(k)
-            if step < TILES:
-                scores_and_exponentials(step)
-            if step >= PRODUCT_LAG:
-                product(step - PRODUCT_LAG)
-            k, rest = divmod(step - QUANTISE_LAG, 4)
-            if rest == 0 and EARLY_CHUNKS <= k < CHUNKS:
-                quantise_e(k)
-            pair, rest = divmod(step - TURN_LAG, 2)
-            if rest == 0 and EARLY_TILES // 2 <= pair < TILES // 2:
-                transpose_pair(pair)
-                copy_pair(pair)
-            if step == EARLY_TILES + 3:
-                quantise_c3p(B - 1)
+        for c in range(2, 14):
+            part = c + 2
+            use_c3(part, 0)
+            done = c // 4 if c % 4 == 2 and c > 2 else None
+            exps_of(c, 0)
+            if done is not None:
+                group_c3p(done, range(0, 2), "s")
+            exps_of(c, 1)
+            if done is not None:
+                group_c3p(done, range(2, 4), "s")
+            use_c3(part, 1)
+            make_c3(part, 2, 3)
+            if c == 2:
+                regroup_piece(5, 0, "s")
+                regroup_piece(5, 1, "g")
+            if part + 2 < 16:
+                regroup_piece(part + 2, 0, "s")
+            exps_of(c, 2)
+            scores_of(c, 3)
+            use_c3(part, 2)
+            make_c3(part, 3, 4)
+            exps_of(c, 3)
+            transposes(c - 1)
+            if c >= 3:
+                store(c - 3)
+            make_c3(part, 4, 3)
+            use_c3(part, 3)
+            if c % 4 == 2:
+                quantise_c3p(c // 4)
+            quantise_e(c - 2)
+            if part + 1 < 16:
+                quantise_x(part + 1)
+            if part + 2 < 16:
+                regroup_piece(part + 2, 1, "s")
+            make_product(c - 2, 0)
+            make_product(c - 2, 1)
+            use_c3(part, 4)
+            use_product(c - 2, 0)
+            make_product(c - 2, 2)
+            if part + 1 < 16:
+                make_c3(part + 1, 0, 3)
+            use_product(c - 2, 1)
+            make_product(c - 2, 3)
+            scores_of(c + 1, 0)
+            scores_of(c + 1, 1)
+            if part + 1 < 16:
+                make_c3(part + 1, 1, 4)
+            scores_of(c + 1, 2)
+            use_product(c - 2, 2)
+            use_product(c - 2, 3)
+
+        def products(k):
+            make_product(k, 0, C3_BANKS)
+            make_product(k, 1, C3_BANKS)
+            for j in range(4):
+                use_product(k, j)
+                if j < 2:
+                    make_product(k, j + 2, C3_BANKS)
+
+        def tail_adds(k):
+            for j in TAIL_VECTOR:
+                add_x(k, j, nc.vector)
+
+        group_c3p(3, range(4), "s")
+        for i in range(4):
+            exps_of(14, i)
+            if i == 0:
+                scores_of(14, 3)
+        scores_of(15, 0)
+        scores_of(15, 1)
+        transposes(13)
+        store(11)
+        scores_of(15, 2)
+        quantise_e(12)
+        quantise_c3p(3)
+        exps_of(15, 0)
+        scores_of(15, 3)
+        exps_of(15, 1)
+        products(12)
+        exps_of(15, 2)
+        transposes(14)
+        exps_of(15, 3)
+        quantise_e(13)
+        tail_adds(12)
+        store(12)
+        products(13)
+        transposes(15)
+        quantise_e(14)
+        tail_adds(13)
+        store(13)
+        products(14)
+        quantise_e(15)
+        tail_adds(14)
+        store(14)
+        products(15)
+        tail_adds(15)
+        for j in range(4):
+            store(15, j)

@@ -31,11 +31,6 @@ PERIODS = CHUNKS + PRODUCT_LAG
 TAIL_VECTOR = (2, 3)
 IN_FLIGHT = 3
 
-SCORE_BANKS = (0, 1, 2)
-C3_BANKS = (3, 4)
-TURN_BANKS = (5, 6)
-ROWS_BANK = 7
-PRODUCT_BANKS = (6, 7)
 
 REGROUP_FIRST = ("vvgs", "sgsv")
 REGROUP_LATER = "sssg"
@@ -46,11 +41,10 @@ def tile_selfspatialattentionmodule_pb_t_kernel(tc, x, c2, c1p, W3, gamma, out):
     with ExitStack() as ctx:
         keep = ctx.enter_context(tc.tile_pool(name="keep", bufs=1))
         work = ctx.enter_context(tc.tile_pool(name="work", bufs=2))
-        psum = ctx.enter_context(tc.psum_pool(name="psum", bufs=1))
-        ctx.enter_context(tc.manual_schedule())
+        psum = ctx.enter_context(tc.psum_pool(name="psum", bufs=8))
 
-        def psum_bank(index, shape, dtype, name):
-            return psum.tile(shape, dtype, name=name, tag="bank%d" % index)
+        def psum_bank(shape, dtype, name):
+            return psum.tile(shape, dtype, name=name, tag="bank")
 
         x_sb = [keep.tile([P, PACK, HALF], BF16, name="x_sb%d" % g) for g in range(HALVES)]
         c2_sb = [keep.tile([P, 2, HALF], BF16, name="c2_sb%d" % g) for g in range(HALVES)]
@@ -97,9 +91,6 @@ def tile_selfspatialattentionmodule_pb_t_kernel(tc, x, c2, c1p, W3, gamma, out):
         nc.vector.memset(warm_in[:], 0.0)
         nc.scalar.activation(out=warm_out[:], in_=warm_in[:], func=ACT.Exp)
         gamma_f32 = keep.tile([P, 1], F32, name="gamma_f32")
-        reciprocals = [keep.tile([P, P], F32, name="reciprocals%d" % i) for i in range(2)]
-        for i in range(2):
-            nc.gpsimd.memset(reciprocals[i][:], 0.0)
 
         def copy_on(engine, dst, src):
             if engine == "v":
@@ -118,7 +109,7 @@ def tile_selfspatialattentionmodule_pb_t_kernel(tc, x, c2, c1p, W3, gamma, out):
         def transpose_w3():
             pairs = w3_sb[:].bitcast(F32).rearrange("p a (q u) -> p a u q", u=2)
             for h in range(2):
-                turned_w3[h] = psum_bank(PRODUCT_BANKS[h], [P, 2, 2, P], F32, "turned_w3")
+                turned_w3[h] = psum_bank([P, 2, 2, P], F32, "turned_w3")
                 for u in range(2):
                     for a in range(2):
                         nc.tensor.transpose(turned_w3[h][:, u, a, :], pairs[:, 2 * h + a, u, :], ident_f32[:])
@@ -175,8 +166,8 @@ def tile_selfspatialattentionmodule_pb_t_kernel(tc, x, c2, c1p, W3, gamma, out):
                 stop=stop,
             )
 
-        def make_c3(part, member, bank):
-            c3[part, member] = psum_bank(bank, [P, C], F32, "c3")
+        def make_c3(part, member):
+            c3[part, member] = psum_bank([P, C], F32, "c3")
             members = range(4) if member == 4 else [member]
             for m in members:
                 step_1_pass(c3[part, member], part, m, m == members[0], m == members[-1])
@@ -227,12 +218,13 @@ def tile_selfspatialattentionmodule_pb_t_kernel(tc, x, c2, c1p, W3, gamma, out):
         spread = {}
         summed = {}
         result = {}
+        reciprocals = {}
         out_view = [out[b].rearrange("(p j) h w -> p j (h w)", j=PACK) for b in range(B)]
 
         def make_scores(t):
             k, i = divmod(t, 4)
             first = (k % 2) * CHUNK + i * P
-            scores[t] = psum_bank(SCORE_BANKS[t % len(SCORE_BANKS)], [P, M], F32, "scores")
+            scores[t] = psum_bank([P, M], F32, "scores")
             for u in range(2):
                 nc.tensor.matmul(
                     out=scores[t][:],
@@ -261,10 +253,11 @@ def tile_selfspatialattentionmodule_pb_t_kernel(tc, x, c2, c1p, W3, gamma, out):
             )
 
         def reciprocal_of_sums(k):
-            nc.vector.reciprocal(out=reciprocals[k % 2][:, 0:4], in_=sums[k][:])
+            reciprocals[k] = work.tile([P, 4], F32, name="reciprocals")
+            nc.vector.reciprocal(out=reciprocals[k][:], in_=sums[k][:])
 
         def transpose_pair(k, second):
-            turned[second] = psum_bank(TURN_BANKS[second], [P, 2, PACK, P], BF16, "turned")
+            turned[second] = psum_bank([P, 2, PACK, P], BF16, "turned")
             for i in range(2):
                 for t in range(PACK):
                     nc.tensor.transpose(
@@ -272,8 +265,11 @@ def tile_selfspatialattentionmodule_pb_t_kernel(tc, x, c2, c1p, W3, gamma, out):
                     )
 
         def transpose_rows(k):
-            rows_psum[0] = psum_bank(ROWS_BANK, [P, P], F32, "rows_psum")
-            nc.tensor.transpose(rows_psum[0][:], reciprocals[k % 2][:], ident_f32[:])
+            rows_psum[0] = psum_bank([P, CHUNK], F32, "rows_psum")
+            for i in range(4):
+                nc.tensor.transpose(
+                    rows_psum[0][:, i * P : (i + 1) * P], reciprocals[k][:, i : i + 1].to_broadcast([P, P]), ident_f32[:]
+                )
 
         def copy_pair(k, second):
             if k not in e_grouped:
@@ -284,7 +280,7 @@ def tile_selfspatialattentionmodule_pb_t_kernel(tc, x, c2, c1p, W3, gamma, out):
             )
 
         def spread_on_chip(k):
-            banks = psum_bank(ROWS_BANK, [P, CHUNK], F32, "spread_psum")
+            banks = psum_bank([P, CHUNK], F32, "spread_psum")
             for i in range(4):
                 nc.tensor.transpose(
                     banks[:, i * P : (i + 1) * P], reciprocals[k % 2][:, i : i + 1].to_broadcast([P, P]), ident_f32[:]
@@ -294,11 +290,7 @@ def tile_selfspatialattentionmodule_pb_t_kernel(tc, x, c2, c1p, W3, gamma, out):
 
         def spread_rows(k):
             spread[k] = work.tile([P, CHUNK], F32, name="spread", bufs=IN_FLIGHT)
-            rows = work.tile([P, P], F32, name="rows")
-            nc.scalar.copy(out=rows[:], in_=rows_psum[0][:])
-            parked = out[B - 1, k, H - CHUNK // W : H, :]
-            nc.sync.dma_start(out=parked.rearrange("(i h) w -> i (h w)", i=4), in_=rows[0:4, :])
-            nc.sync.dma_start(out=spread[k][:], in_=parked.rearrange("h w -> (h w)").partition_broadcast(P))
+            nc.scalar.copy(out=spread[k][:], in_=rows_psum[0][:])
 
         def quantise_e(k):
             e_words[k] = work.tile([P, CHUNK], U32, name="e_words", bufs=IN_FLIGHT, align_bytes=64)
@@ -307,9 +299,9 @@ def tile_selfspatialattentionmodule_pb_t_kernel(tc, x, c2, c1p, W3, gamma, out):
                 out=e_words[k][:].bitcast(FP8X4), scales=e_scales[k][:], in_=e_grouped[k][:].rearrange("p n t -> p (n t)")
             )
 
-        def make_product(k, j, banks=PRODUCT_BANKS):
+        def make_product(k, j):
             b = k // 4
-            summed[k, j] = psum_bank(banks[(j + 1) % 2], [P, CHUNK], F32, "summed")
+            summed[k, j] = psum_bank([P, CHUNK], F32, "summed")
             nc.tensor.matmul_mx(
                 out=summed[k, j][:],
                 lhsT=c3p_words[b][:, j * P : (j + 1) * P].bitcast(FP8X4),
@@ -350,196 +342,137 @@ def tile_selfspatialattentionmodule_pb_t_kernel(tc, x, c2, c1p, W3, gamma, out):
             else:
                 nc.sync.dma_start(out=out_view[b][:, j, pixels], in_=result[k][:, j, :])
 
-        def scores_of(c, i):
-            if c < CHUNKS:
-                make_scores(4 * c + i)
+        def score(c, i):
+            make_scores(4 * c + i)
+            use_scores(4 * c + i)
 
-        def exps_of(c, i):
-            if c < CHUNKS:
-                use_scores(4 * c + i)
+        def pooled(part, member):
+            make_c3(part, member)
+            use_c3(part, member)
 
-        bank_count = [0]
-
-        def ring5(part, member):
-            make_c3(part, member, 3 + bank_count[0] % 5)
-            bank_count[0] += 1
+        def products(k, tail=False):
+            for j in range(4):
+                make_product(k, j)
+                use_product(k, j)
 
         def transposes(k):
-            reciprocal_of_sums(k)
             transpose_pair(k, 0)
             transpose_pair(k, 1)
-            if k < CHUNKS - 1:
-                transpose_rows(k)
-                spread_rows(k)
-            else:
-                spread_on_chip(k)
-            copy_pair(k, 1)
+            transpose_rows(k)
             copy_pair(k, 0)
-
-        scores_of(0, 0)
-        scores_of(0, 1)
-        transpose_w3()
-        scores_of(0, 2)
-        exps_of(0, 0)
-        copy_w3(0, "s")
-        copy_w3(1, "s")
-        exps_of(0, 1)
-        scores_of(0, 3)
-        regroup_piece(0, 0, "v")
-        regroup_piece(0, 1, "v")
-        regroup_piece(1, 0, "s")
-        exps_of(0, 2)
-        quantise_w3()
-        quantise_x(0)
-        for member in range(3):
-            ring5(0, member)
-        use_c3(0, 0)
-        regroup_piece(1, 1, "s")
-        exps_of(0, 3)
-        scores_of(1, 0)
-        ring5(0, 3)
-        ring5(0, 4)
-        regroup_piece(2, 0, "g")
-        regroup_piece(2, 1, "g")
-        scores_of(1, 1)
-        use_c3(0, 1)
-        exps_of(1, 0)
-        use_c3(0, 2)
-        quantise_x(1)
-        use_c3(0, 3)
-        for member in range(3):
-            ring5(1, member)
-        use_c3(1, 0)
-        exps_of(1, 1)
-        scores_of(1, 2)
-        use_c3(0, 4)
-        use_c3(1, 1)
-        ring5(1, 3)
-        ring5(1, 4)
-        quantise_x(2)
-        regroup_piece(3, 0, "g")
-        regroup_piece(3, 1, "s")
-        for member in range(3):
-            ring5(2, member)
-        use_c3(2, 0)
-        use_c3(1, 2)
-        exps_of(1, 2)
-        scores_of(1, 3)
-        use_c3(1, 3)
-        use_c3(2, 1)
-        ring5(2, 3)
-        ring5(2, 4)
-        regroup_piece(4, 0, "s")
-        use_c3(1, 4)
-        quantise_x(3)
-        use_c3(2, 2)
-        scores_of(2, 0)
-        for member in range(3):
-            ring5(3, member)
-        use_c3(3, 0)
-        exps_of(1, 3)
-        regroup_piece(4, 1, "g")
-        use_c3(2, 3)
-        use_c3(3, 1)
-        ring5(3, 3)
-        ring5(3, 4)
-        use_c3(2, 4)
-        use_c3(3, 2)
-        scores_of(2, 1)
-        quantise_x(4)
-        make_c3(4, 0, 3)
-        use_c3(3, 3)
-        transposes(0)
-        make_c3(4, 1, 4)
-        use_c3(3, 4)
-        group_c3p(0, range(4), "g")
-        scores_of(2, 2)
-        nc.vector.tensor_copy(out=gamma_f32[:], in_=gamma_bf[:])
-        for c in range(2, 14):
-            part = c + 2
-            use_c3(part, 0)
-            done = c // 4 if c % 4 == 2 and c > 2 else None
-            exps_of(c, 0)
-            if done is not None:
-                group_c3p(done, range(0, 2), "s")
-            exps_of(c, 1)
-            if done is not None:
-                group_c3p(done, range(2, 4), "s")
-            use_c3(part, 1)
-            make_c3(part, 2, 3)
-            if c == 2:
-                regroup_piece(5, 0, "s")
-                regroup_piece(5, 1, "g")
-            if part + 2 < 16:
-                regroup_piece(part + 2, 0, "s")
-            exps_of(c, 2)
-            scores_of(c, 3)
-            use_c3(part, 2)
-            make_c3(part, 3, 4)
-            exps_of(c, 3)
-            transposes(c - 1)
-            if c >= 3:
-                store(c - 3)
-            make_c3(part, 4, 3)
-            use_c3(part, 3)
-            if c % 4 == 2:
-                quantise_c3p(c // 4)
-            quantise_e(c - 2)
-            if part + 1 < 16:
-                quantise_x(part + 1)
-            if part + 2 < 16:
-                regroup_piece(part + 2, 1, "s")
-            make_product(c - 2, 0)
-            make_product(c - 2, 1)
-            use_c3(part, 4)
-            use_product(c - 2, 0)
-            make_product(c - 2, 2)
-            if part + 1 < 16:
-                make_c3(part + 1, 0, 3)
-            use_product(c - 2, 1)
-            make_product(c - 2, 3)
-            scores_of(c + 1, 0)
-            scores_of(c + 1, 1)
-            if part + 1 < 16:
-                make_c3(part + 1, 1, 4)
-            scores_of(c + 1, 2)
-            use_product(c - 2, 2)
-            use_product(c - 2, 3)
-
-        def products(k):
-            make_product(k, 0, C3_BANKS)
-            make_product(k, 1, C3_BANKS)
-            for j in range(4):
-                use_product(k, j)
-                if j < 2:
-                    make_product(k, j + 2, C3_BANKS)
+            copy_pair(k, 1)
+            spread_rows(k)
 
         def tail_adds(k):
             for j in TAIL_VECTOR:
                 add_x(k, j, nc.vector)
 
+        score(0, 0)
+        transpose_w3()
+        score(0, 1)
+        copy_w3(0, "s")
+        copy_w3(1, "s")
+        regroup_piece(0, 0, "v")
+        regroup_piece(0, 1, "v")
+        score(0, 2)
+        regroup_piece(1, 0, "s")
+        quantise_w3()
+        quantise_x(0)
+        pooled(0, 0)
+        score(0, 3)
+        regroup_piece(1, 1, "s")
+        regroup_piece(2, 0, "g")
+        regroup_piece(2, 1, "g")
+        score(1, 0)
+        pooled(0, 1)
+        score(1, 1)
+        pooled(0, 2)
+        quantise_x(1)
+        pooled(1, 0)
+        pooled(0, 3)
+        regroup_piece(3, 0, "g")
+        regroup_piece(3, 1, "s")
+        pooled(1, 1)
+        pooled(0, 4)
+        pooled(1, 2)
+        quantise_x(2)
+        pooled(2, 0)
+        pooled(1, 3)
+        score(1, 2)
+        pooled(2, 1)
+        pooled(1, 4)
+        regroup_piece(4, 0, "s")
+        regroup_piece(4, 1, "g")
+        pooled(2, 2)
+        quantise_x(3)
+        pooled(3, 0)
+        pooled(2, 3)
+        score(1, 3)
+        pooled(3, 1)
+        pooled(2, 4)
+        reciprocal_of_sums(0)
+        pooled(3, 2)
+        regroup_piece(5, 0, "s")
+        regroup_piece(5, 1, "s")
+        quantise_x(4)
+        transposes(0)
+        pooled(3, 3)
+        pooled(4, 0)
+        score(2, 0)
+        pooled(3, 4)
+        group_c3p(0, range(4), "g")
+        nc.vector.tensor_copy(out=gamma_f32[:], in_=gamma_bf[:])
+        for c in range(2, 14):
+            part = c + 2
+            done = c // 4 if c % 4 == 2 and c > 2 else None
+            if c > 2:
+                pooled(part, 0)
+                score(c, 0)
+            if done is not None:
+                group_c3p(done, range(0, 2), "s")
+            score(c, 1)
+            if done is not None:
+                group_c3p(done, range(2, 4), "s")
+            reciprocal_of_sums(c - 1)
+            pooled(part, 1)
+            if part + 2 < 16:
+                regroup_piece(part + 2, 0, "s")
+            score(c, 2)
+            pooled(part, 2)
+            score(c, 3)
+            pooled(part, 3)
+            if c >= 3:
+                store(c - 3)
+            if c % 4 == 2:
+                quantise_c3p(c // 4)
+            quantise_e(c - 2)
+            transposes(c - 1)
+            if part + 1 < 16:
+                quantise_x(part + 1)
+            if part + 2 < 16:
+                regroup_piece(part + 2, 1, "s")
+            pooled(part, 4)
+            products(c - 2)
+
         group_c3p(3, range(4), "s")
+        reciprocal_of_sums(13)
         for i in range(4):
-            exps_of(14, i)
-            if i == 0:
-                scores_of(14, 3)
-        scores_of(15, 0)
-        scores_of(15, 1)
+            score(14, i)
         transposes(13)
         store(11)
-        scores_of(15, 2)
         quantise_e(12)
         quantise_c3p(3)
-        exps_of(15, 0)
-        scores_of(15, 3)
-        exps_of(15, 1)
+        score(15, 0)
+        score(15, 1)
+        reciprocal_of_sums(14)
         products(12)
-        exps_of(15, 2)
         transposes(14)
-        exps_of(15, 3)
+        score(15, 2)
+        score(15, 3)
         quantise_e(13)
         tail_adds(12)
         store(12)
+        reciprocal_of_sums(15)
         products(13)
         transposes(15)
         quantise_e(14)

@@ -52,9 +52,6 @@ def tile_selfspatialattentionmodule_pb_t_kernel(tc, x, c2, c1p, W3, gamma, out):
         w3_sb = keep.tile([P, PACK, C], BF16, name="w3_sb")
         gamma_bf = keep.tile([P, 1], BF16, name="gamma_bf")
 
-        def pixels_of_half(g):
-            return slice((g % 2) * HALF, (g % 2 + 1) * HALF)
-
         def load_x(g, pieces=1):
             view = x[g // 2].rearrange("(p j) h w -> p j (h w)", j=PACK)
             width = HALF // pieces
@@ -62,25 +59,28 @@ def tile_selfspatialattentionmodule_pb_t_kernel(tc, x, c2, c1p, W3, gamma, out):
                 start = (g % 2) * HALF + first
                 nc.sync.dma_start(out=x_sb[g][:, :, first : first + width], in_=view[:, :, start : start + width])
 
-        def load_c2(g):
+        def load_c2(g, first=0, width=HALF):
             view = c2[g // 2].rearrange("(u p) h w -> p u (h w)", u=2)
-            nc.sync.dma_start(out=c2_sb[g][:], in_=view[:, :, pixels_of_half(g)])
+            start = (g % 2) * HALF + first
+            nc.sync.dma_start(out=c2_sb[g][:, :, first : first + width], in_=view[:, :, start : start + width])
 
         def load_c1(b):
             nc.sync.dma_start(out=c1_sb[b][:], in_=c1p[b].rearrange("(u p) i j -> p u (i j)", u=2))
 
         load_c1(0)
-        load_c2(0)
+        load_c2(0, 0, CHUNK)
         nc.sync.dma_start(out=w3_sb[:], in_=W3.rearrange("(p a) i -> p a i", a=PACK))
         load_x(0, 2)
+        load_c2(0, CHUNK, CHUNK)
         load_x(1)
-        nc.sync.dma_start(out=gamma_bf[:], in_=gamma.partition_broadcast(P))
         load_c2(1)
         for g in range(2, HALVES):
             load_x(g)
             if g % 2 == 0:
                 load_c1(g // 2)
             load_c2(g)
+            if g == 3:
+                nc.sync.dma_start(out=gamma_bf[:], in_=gamma.partition_broadcast(P))
 
         ident_bf = keep.tile([P, P], BF16, name="ident_bf")
         make_identity(nc, ident_bf[:])
@@ -239,7 +239,7 @@ def tile_selfspatialattentionmodule_pb_t_kernel(tc, x, c2, c1p, W3, gamma, out):
             if i == 0:
                 negative_max[k] = work.tile([P, 4], F32, name="negative_max", bufs=IN_FLIGHT)
                 sums[k] = work.tile([P, 4], F32, name="sums", bufs=IN_FLIGHT)
-                e_bf[k] = work.tile([P, 4, M], BF16, name="e_bf", bufs=IN_FLIGHT)
+                e_bf[k] = work.tile([P, 4, M], BF16, name="e_bf", bufs=3)
             nc.vector.tensor_reduce(
                 out=negative_max[k][:, i : i + 1], in_=scores[t][:], axis=AX.X, op=ALU.max, negate=True
             )
@@ -323,8 +323,11 @@ def tile_selfspatialattentionmodule_pb_t_kernel(tc, x, c2, c1p, W3, gamma, out):
                 op0=ALU.mult,
                 op1=ALU.mult,
             )
-            if k < 12 or j not in TAIL_VECTOR:
+            if j not in vector_adds(k):
                 add_x(k, j, nc.gpsimd)
+
+        def vector_adds(k):
+            return () if k < 12 else (2, 3)
 
         def add_x(k, j, engine):
             engine.tensor_tensor(
@@ -364,7 +367,7 @@ def tile_selfspatialattentionmodule_pb_t_kernel(tc, x, c2, c1p, W3, gamma, out):
             spread_rows(k)
 
         def tail_adds(k):
-            for j in TAIL_VECTOR:
+            for j in vector_adds(k):
                 add_x(k, j, nc.vector)
 
         score(0, 0)
@@ -382,7 +385,7 @@ def tile_selfspatialattentionmodule_pb_t_kernel(tc, x, c2, c1p, W3, gamma, out):
         score(0, 3)
         regroup_piece(1, 1, "s")
         regroup_piece(2, 0, "g")
-        regroup_piece(2, 1, "g")
+        regroup_piece(2, 1, "s")
         score(1, 0)
         pooled(0, 1)
         score(1, 1)
@@ -401,8 +404,8 @@ def tile_selfspatialattentionmodule_pb_t_kernel(tc, x, c2, c1p, W3, gamma, out):
         score(1, 2)
         pooled(2, 1)
         pooled(1, 4)
-        regroup_piece(4, 0, "s")
-        regroup_piece(4, 1, "g")
+        regroup_piece(4, 0, "g")
+        regroup_piece(4, 1, "s")
         pooled(2, 2)
         quantise_x(3)
         pooled(3, 0)
@@ -412,7 +415,7 @@ def tile_selfspatialattentionmodule_pb_t_kernel(tc, x, c2, c1p, W3, gamma, out):
         pooled(2, 4)
         reciprocal_of_sums(0)
         pooled(3, 2)
-        regroup_piece(5, 0, "s")
+        regroup_piece(5, 0, "g")
         regroup_piece(5, 1, "s")
         quantise_x(4)
         transposes(0)

@@ -49,6 +49,7 @@ def tile_selfspatialattentionmodule_pb_t_kernel(tc, x, c2, c1p, W3, gamma, out):
         x_sb = [keep.tile([P, PACK, HALF], BF16, name="x_sb%d" % g) for g in range(HALVES)]
         c2_sb = [keep.tile([P, 2, HALF], BF16, name="c2_sb%d" % g) for g in range(HALVES)]
         c1_sb = [keep.tile([P, 2, M], BF16, name="c1_sb%d" % b) for b in range(B)]
+        c1_paired = [keep.tile([P, 2, M], BF16, name="c1_paired%d" % b) for b in range(B)]
         w3_sb = keep.tile([P, PACK, C], BF16, name="w3_sb")
         gamma_bf = keep.tile([P, 1], BF16, name="gamma_bf")
 
@@ -82,8 +83,6 @@ def tile_selfspatialattentionmodule_pb_t_kernel(tc, x, c2, c1p, W3, gamma, out):
             if g == 3:
                 nc.sync.dma_start(out=gamma_bf[:], in_=gamma.partition_broadcast(P))
 
-        ident_bf = keep.tile([P, P], BF16, name="ident_bf")
-        make_identity(nc, ident_bf[:])
         ident_f32 = keep.tile([P, P], F32, name="ident_f32")
         make_identity(nc, ident_f32[:])
         warm_in = keep.tile([P, 1], F32, name="warm_in")
@@ -99,6 +98,13 @@ def tile_selfspatialattentionmodule_pb_t_kernel(tc, x, c2, c1p, W3, gamma, out):
                 nc.scalar.copy(out=dst, in_=src)
             else:
                 nc.gpsimd.tensor_scalar(out=dst, in0=src, scalar1=1.0, scalar2=0.0, op0=ALU.mult, op1=ALU.add)
+
+        def pair_c1(b, engine):
+            copy_on(
+                engine,
+                c1_paired[b][:].rearrange("p u (h q e) -> p (u h) q e", h=2, e=2),
+                c1_sb[b][:].rearrange("p u (h e q) -> p (u h) q e", h=2, e=2),
+            )
 
         w3_grouped = keep.tile([P, C, PACK], BF16, name="w3_grouped", align_bytes=64)
         w3_words = keep.tile([P, C], U32, name="w3_words", align_bytes=64)
@@ -229,7 +235,7 @@ def tile_selfspatialattentionmodule_pb_t_kernel(tc, x, c2, c1p, W3, gamma, out):
                 nc.tensor.matmul(
                     out=scores[t][:],
                     lhsT=c2_sb[k // 2][:, u, first : first + P],
-                    rhs=c1_sb[k // 4][:, u, :],
+                    rhs=c1_paired[k // 4][:, u, :],
                     start=u == 0,
                     stop=u == 1,
                 )
@@ -257,11 +263,12 @@ def tile_selfspatialattentionmodule_pb_t_kernel(tc, x, c2, c1p, W3, gamma, out):
             nc.vector.reciprocal(out=reciprocals[k][:], in_=sums[k][:])
 
         def transpose_pair(k, second):
-            turned[second] = psum_bank([P, 2, PACK, P], BF16, "turned")
+            turned[second] = psum_bank([P, 2, 2, P], F32, "turned")
+            words = e_bf[k][:].bitcast(F32)
             for i in range(2):
-                for t in range(PACK):
+                for h in range(2):
                     nc.tensor.transpose(
-                        turned[second][:, i, t, :], e_bf[k][:, 2 * second + i, t * P : (t + 1) * P], ident_bf[:]
+                        turned[second][:, i, h, :], words[:, 2 * second + i, h * P : (h + 1) * P], ident_f32[:]
                     )
 
         def transpose_rows(k):
@@ -274,9 +281,10 @@ def tile_selfspatialattentionmodule_pb_t_kernel(tc, x, c2, c1p, W3, gamma, out):
         def copy_pair(k, second):
             if k not in e_grouped:
                 e_grouped[k] = work.tile([P, CHUNK, PACK], BF16, name="e_grouped", align_bytes=64)
-            nc.scalar.copy(
-                out=e_grouped[k][:, 2 * P * second : 2 * P * (second + 1), :].rearrange("p (i n) t -> p i n t", i=2),
-                in_=turned[second][:].rearrange("p i t n -> p i n t"),
+            copy_on(
+                "s",
+                e_grouped[k][:].bitcast(F32)[:, 2 * P * second : 2 * P * (second + 1), :].rearrange("p (i n) h -> p i n h", i=2),
+                turned[second][:].rearrange("p i h n -> p i n h"),
             )
 
         def spread_on_chip(k):
@@ -327,7 +335,7 @@ def tile_selfspatialattentionmodule_pb_t_kernel(tc, x, c2, c1p, W3, gamma, out):
                 add_x(k, j, nc.gpsimd)
 
         def vector_adds(k):
-            return () if k < 12 else (2, 3)
+            return () if k < 12 else (1, 2, 3) if k == 15 else (2, 3)
 
         def add_x(k, j, engine):
             engine.tensor_tensor(
@@ -370,6 +378,7 @@ def tile_selfspatialattentionmodule_pb_t_kernel(tc, x, c2, c1p, W3, gamma, out):
             for j in vector_adds(k):
                 add_x(k, j, nc.vector)
 
+        pair_c1(0, "v")
         score(0, 0)
         transpose_w3()
         score(0, 1)
@@ -446,6 +455,8 @@ def tile_selfspatialattentionmodule_pb_t_kernel(tc, x, c2, c1p, W3, gamma, out):
             pooled(part, 3)
             if c >= 3:
                 store(c - 3)
+            if c % 4 == 2 and c < 13:
+                pair_c1((c + 2) // 4, "s")
             if c % 4 == 2:
                 quantise_c3p(c // 4)
             quantise_e(c - 2)

@@ -189,14 +189,21 @@ def tile_selfspatialattentionmodule_pb_t_kernel(tc, x, c2, c1p, W3, gamma, out):
                 b, plane = divmod(part, 4)
                 if plane == 0:
                     c3p_planes[b] = work.tile([P, PACK, C], BF16, name="c3p_planes")
-                nc.vector.scalar_tensor_tensor(
-                    out=c3p_planes[b][:, plane, :],
-                    in0=read[:],
-                    scalar=0.25,
-                    in1=largest[part][:],
-                    op0=ALU.mult,
-                    op1=ALU.add,
-                )
+                if part % 4 < 2:
+                    mean = work.tile([P, C], F32, name="mean", bufs=1)
+                    nc.scalar.activation(out=mean[:], in_=read[:], func=ACT.Copy, scale=0.25)
+                    nc.gpsimd.tensor_tensor(
+                        out=c3p_planes[b][:, plane, :], in0=mean[:], in1=largest[part][:], op=ALU.add
+                    )
+                else:
+                    nc.vector.scalar_tensor_tensor(
+                        out=c3p_planes[b][:, plane, :],
+                        in0=read[:],
+                        scalar=0.25,
+                        in1=largest[part][:],
+                        op0=ALU.mult,
+                        op1=ALU.add,
+                    )
 
         def group_c3p(b, quarters, engine):
             if b not in c3p_grouped:
@@ -335,7 +342,7 @@ def tile_selfspatialattentionmodule_pb_t_kernel(tc, x, c2, c1p, W3, gamma, out):
                 add_x(k, j, nc.gpsimd)
 
         def vector_adds(k):
-            return () if k < 12 else (1, 2, 3) if k == 15 else (2, 3)
+            return () if k < 13 else (1, 2, 3) if k == 15 else (2, 3)
 
         def add_x(k, j, engine):
             engine.tensor_tensor(
@@ -394,7 +401,7 @@ def tile_selfspatialattentionmodule_pb_t_kernel(tc, x, c2, c1p, W3, gamma, out):
         score(0, 3)
         regroup_piece(1, 1, "s")
         regroup_piece(2, 0, "g")
-        regroup_piece(2, 1, "s")
+        regroup_piece(2, 1, "g")
         score(1, 0)
         pooled(0, 1)
         score(1, 1)
@@ -402,7 +409,7 @@ def tile_selfspatialattentionmodule_pb_t_kernel(tc, x, c2, c1p, W3, gamma, out):
         quantise_x(1)
         pooled(1, 0)
         pooled(0, 3)
-        regroup_piece(3, 0, "g")
+        regroup_piece(3, 0, "s")
         regroup_piece(3, 1, "s")
         pooled(1, 1)
         pooled(0, 4)
@@ -425,7 +432,7 @@ def tile_selfspatialattentionmodule_pb_t_kernel(tc, x, c2, c1p, W3, gamma, out):
         reciprocal_of_sums(0)
         pooled(3, 2)
         regroup_piece(5, 0, "g")
-        regroup_piece(5, 1, "s")
+        regroup_piece(5, 1, "g")
         quantise_x(4)
         transposes(0)
         pooled(3, 3)

from contextlib import ExitStack

import concourse.mybir as mybir
from concourse.masks import make_identity

F32 = mybir.dt.float32
BF16 = mybir.dt.bfloat16
U32 = mybir.dt.uint32
U8 = mybir.dt.uint8
FP8X4 = mybir.dt.float8_e4m3fn_x4
ALU = mybir.AluOpType
ACT = mybir.ActivationFunctionType
AX = mybir.AxisListType

B, C, H, W = 4, 512, 64, 32
CH = C // 2
N = H * W
M = (H // 2) * (W // 2)
FLOPS = 2 * B * (C * C * N + CH * N * M + C * M * N)

P = 128
PACK = 4
HALF = N // 2
HALVES = 2 * B
POOLED = HALF // 4
CHUNK = 4 * P
TILES = B * N // P
CHUNKS = TILES // 4
PRODUCT_LAG = 2
PERIODS = CHUNKS + PRODUCT_LAG
TAIL_VECTOR = (2, 3)
IN_FLIGHT = 3


REGROUP_FIRST = ("vvgs", "sgsv")
REGROUP_LATER = "sssg"


def tile_selfspatialattentionmodule_pb_t_kernel(tc, x, c2, c1p, W3, gamma, out):
    nc = tc.nc
    with ExitStack() as ctx:
        keep = ctx.enter_context(tc.tile_pool(name="keep", bufs=1))
        work = ctx.enter_context(tc.tile_pool(name="work", bufs=2))
        psum = ctx.enter_context(tc.psum_pool(name="psum", bufs=8))

        def psum_bank(shape, dtype, name):
            return psum.tile(shape, dtype, name=name, tag="bank")

        x_sb = [keep.tile([P, PACK, HALF], BF16, name="x_sb%d" % g) for g in range(HALVES)]
        c2_sb = [keep.tile([P, 2, HALF], BF16, name="c2_sb%d" % g) for g in range(HALVES)]
        c1_sb = [keep.tile([P, 2, M], BF16, name="c1_sb%d" % b) for b in range(B)]
        c1_paired = [keep.tile([P, 2, M], BF16, name="c1_paired%d" % b) for b in range(B)]
        w3_sb = keep.tile([P, PACK, C], BF16, name="w3_sb")
        gamma_bf = keep.tile([P, 1], BF16, name="gamma_bf")

        def load_x(g, pieces=1):
            view = x[g // 2].rearrange("(p j) h w -> p j (h w)", j=PACK)
            width = HALF // pieces
            for first in range(0, HALF, width):
                start = (g % 2) * HALF + first
                nc.sync.dma_start(out=x_sb[g][:, :, first : first + width], in_=view[:, :, start : start + width])

        def load_c2(g, first=0, width=HALF):
            view = c2[g // 2].rearrange("(u p) h w -> p u (h w)", u=2)
            start = (g % 2) * HALF + first
            nc.sync.dma_start(out=c2_sb[g][:, :, first : first + width], in_=view[:, :, start : start + width])

        def load_c1(b):
            nc.sync.dma_start(out=c1_sb[b][:], in_=c1p[b].rearrange("(u p) i j -> p u (i j)", u=2))

        load_c1(0)
        load_c2(0, 0, CHUNK)
        nc.sync.dma_start(out=w3_sb[:], in_=W3.rearrange("(p a) i -> p a i", a=PACK))
        load_x(0, 2)
        load_c2(0, CHUNK, CHUNK)
        load_x(1)
        load_c2(1)
        for g in range(2, HALVES):
            load_x(g)
            if g % 2 == 0:
                load_c1(g // 2)
            load_c2(g)
            if g == 3:
                nc.sync.dma_start(out=gamma_bf[:], in_=gamma.partition_broadcast(P))

        ident_f32 = keep.tile([P, P], F32, name="ident_f32")
        make_identity(nc, ident_f32[:])
        warm_in = keep.tile([P, 1], F32, name="warm_in")
        warm_out = keep.tile([P, 1], F32, name="warm_out")
        nc.vector.memset(warm_in[:], 0.0)
        nc.scalar.activation(out=warm_out[:], in_=warm_in[:], func=ACT.Exp)
        gamma_f32 = keep.tile([P, 1], F32, name="gamma_f32")

        def copy_on(engine, dst, src):
            if engine == "v":
                nc.vector.tensor_copy(out=dst, in_=src)
            elif engine == "s":
                nc.scalar.copy(out=dst, in_=src)
            else:
                nc.gpsimd.tensor_scalar(out=dst, in0=src, scalar1=1.0, scalar2=0.0, op0=ALU.mult, op1=ALU.add)

        def pair_c1(b, engine):
            copy_on(
                engine,
                c1_paired[b][:].rearrange("p u (h q e) -> p (u h) q e", h=2, e=2),
                c1_sb[b][:].rearrange("p u (h e q) -> p (u h) q e", h=2, e=2),
            )

        w3_grouped = keep.tile([P, C, PACK], BF16, name="w3_grouped", align_bytes=64)
        w3_words = keep.tile([P, C], U32, name="w3_words", align_bytes=64)
        w3_scales = keep.tile([P, C], U8, name="w3_scales", align_bytes=64)

        turned_w3 = {}

        def transpose_w3():
            pairs = w3_sb[:].bitcast(F32).rearrange("p a (q u) -> p a u q", u=2)
            for h in range(2):
                turned_w3[h] = psum_bank([P, 2, 2, P], F32, "turned_w3")
                for u in range(2):
                    for a in range(2):
                        nc.tensor.transpose(turned_w3[h][:, u, a, :], pairs[:, 2 * h + a, u, :], ident_f32[:])

        def copy_w3(h, engine):
            copy_on(
                engine,
                w3_grouped[:].bitcast(F32)[:, 2 * P * h : 2 * P * (h + 1), :].rearrange("p (a q) u -> p a q u", a=2),
                turned_w3[h][:].rearrange("p u a q -> p a q u"),
            )

        def quantise_w3():
            nc.vector.quantize_mx(
                out=w3_words[:].bitcast(FP8X4), scales=w3_scales[:], in_=w3_grouped[:].rearrange("p c j -> p (c j)")
            )

        x_grouped = {}
        x_words = {}
        x_scales = {}

        def regroup_piece(part, dh, engine):
            if part not in x_grouped:
                x_grouped[part] = work.tile([P, 4, P, PACK], BF16, name="x_grouped", bufs=3, align_bytes=64)
            g, rows = divmod(part, 2)
            src = x_sb[g][:].rearrange("p j (i dh jj dw) -> p dh i jj dw j", i=16, dh=2, jj=16, dw=2)
            dst = x_grouped[part][:, 2 * dh : 2 * dh + 2, :, :]
            copy_on(engine, dst.rearrange("p dw (i jj) j -> p i jj dw j", i=8), src[:, dh, 8 * rows : 8 * (rows + 1)])

        def quantise_x(part):
            x_words[part] = work.tile([P, 4 * P], U32, name="x_words", bufs=3, align_bytes=64)
            x_scales[part] = work.tile([P, 4 * P], U8, name="x_scales", bufs=3, align_bytes=64)
            nc.vector.quantize_mx(
                out=x_words[part][:].bitcast(FP8X4),
                scales=x_scales[part][:],
                in_=x_grouped[part][:].rearrange("p m q j -> p (m q j)"),
            )

        c3p_words = [keep.tile([P, C], U32, name="c3p_words%d" % b, align_bytes=64) for b in range(B)]
        c3p_scales = [keep.tile([P, C], U8, name="c3p_scales%d" % b, align_bytes=64) for b in range(B)]
        c3p_planes = {}
        c3p_grouped = {}
        c3 = {}
        largest = {}

        def step_1_pass(dst, part, member, start, stop):
            cols = slice(member * P, (member + 1) * P)
            nc.tensor.matmul_mx(
                out=dst[:],
                lhsT=x_words[part][:, cols].bitcast(FP8X4),
                lhsT_scale=x_scales[part][:, cols],
                rhs=w3_words[:].bitcast(FP8X4),
                rhs_scale=w3_scales[:],
                start=start,
                stop=stop,
            )

        def make_c3(part, member):
            c3[part, member] = psum_bank([P, C], F32, "c3")
            members = range(4) if member == 4 else [member]
            for m in members:
                step_1_pass(c3[part, member], part, m, m == members[0], m == members[-1])

        def use_c3(part, member):
            read = c3[part, member]
            if member == 0:
                largest[part] = work.tile([P, C], F32, name="largest", bufs=3)
                nc.scalar.copy(out=largest[part][:], in_=read[:])
            elif member < 4:
                nc.vector.tensor_tensor(out=largest[part][:], in0=largest[part][:], in1=read[:], op=ALU.max)
            else:
                b, plane = divmod(part, 4)
                if plane == 0:
                    c3p_planes[b] = work.tile([P, PACK, C], BF16, name="c3p_planes")
                if part % 4 < 2:
                    mean = work.tile([P, C], F32, name="mean", bufs=1)
                    nc.scalar.activation(out=mean[:], in_=read[:], func=ACT.Copy, scale=0.25)
                    nc.gpsimd.tensor_tensor(
                        out=c3p_planes[b][:, plane, :], in0=mean[:], in1=largest[part][:], op=ALU.add
                    )
                else:
                    nc.vector.scalar_tensor_tensor(
                        out=c3p_planes[b][:, plane, :],
                        in0=read[:],
                        scalar=0.25,
                        in1=largest[part][:],
                        op0=ALU.mult,
                        op1=ALU.add,
                    )

        def group_c3p(b, quarters, engine):
            if b not in c3p_grouped:
                c3p_grouped[b] = work.tile([P, C, PACK], BF16, name="c3p_grouped", bufs=1, align_bytes=64)
            for quarter in quarters:
                channels = slice(quarter * P, (quarter + 1) * P)
                copy_on(engine, c3p_grouped[b][:, channels, :], c3p_planes[b][:, :, channels].rearrange("p t c -> p c t"))

        def quantise_c3p(b):
            nc.vector.quantize_mx(
                out=c3p_words[b][:].bitcast(FP8X4),
                scales=c3p_scales[b][:],
                in_=c3p_grouped[b][:].rearrange("p c t -> p (c t)"),
            )

        scores = {}
        negative_max = {}
        sums = {}
        e_bf = {}
        turned = {}
        rows_psum = {}
        e_grouped = {}
        e_words = {}
        e_scales = {}
        spread = {}
        summed = {}
        result = {}
        reciprocals = {}
        out_view = [out[b].rearrange("(p j) h w -> p j (h w)", j=PACK) for b in range(B)]

        def make_scores(t):
            k, i = divmod(t, 4)
            first = (k % 2) * CHUNK + i * P
            scores[t] = psum_bank([P, M], F32, "scores")
            for u in range(2):
                nc.tensor.matmul(
                    out=scores[t][:],
                    lhsT=c2_sb[k // 2][:, u, first : first + P],
                    rhs=c1_paired[k // 4][:, u, :],
                    start=u == 0,
                    stop=u == 1,
                )

        def use_scores(t):
            k, i = divmod(t, 4)
            if i == 0:
                negative_max[k] = work.tile([P, 4], F32, name="negative_max", bufs=IN_FLIGHT)
                sums[k] = work.tile([P, 4], F32, name="sums", bufs=IN_FLIGHT)
                e_bf[k] = work.tile([P, 4, M], BF16, name="e_bf", bufs=3)
            nc.vector.tensor_reduce(
                out=negative_max[k][:, i : i + 1], in_=scores[t][:], axis=AX.X, op=ALU.max, negate=True
            )
            nc.scalar.activation(
                out=e_bf[k][:, i, :],
                in_=scores[t][:],
                func=ACT.Exp,
                bias=negative_max[k][:, i : i + 1],
                scale=1.0,
                accum_out=sums[k][:, i : i + 1],
            )

        def reciprocal_of_sums(k):
            reciprocals[k] = work.tile([P, 4], F32, name="reciprocals")
            nc.vector.reciprocal(out=reciprocals[k][:], in_=sums[k][:])

        def transpose_pair(k, second):
            turned[second] = psum_bank([P, 2, 2, P], F32, "turned")
            words = e_bf[k][:].bitcast(F32)
            for i in range(2):
                for h in range(2):
                    nc.tensor.transpose(
                        turned[second][:, i, h, :], words[:, 2 * second + i, h * P : (h + 1) * P], ident_f32[:]
                    )

        def transpose_rows(k):
            rows_psum[0] = psum_bank([P, CHUNK], F32, "rows_psum")
            for i in range(4):
                nc.tensor.transpose(
                    rows_psum[0][:, i * P : (i + 1) * P], reciprocals[k][:, i : i + 1].to_broadcast([P, P]), ident_f32[:]
                )

        def copy_pair(k, second):
            if k not in e_grouped:
                e_grouped[k] = work.tile([P, CHUNK, PACK], BF16, name="e_grouped", align_bytes=64)
            copy_on(
                "s",
                e_grouped[k][:].bitcast(F32)[:, 2 * P * second : 2 * P * (second + 1), :].rearrange("p (i n) h -> p i n h", i=2),
                turned[second][:].rearrange("p i h n -> p i n h"),
            )

        def spread_on_chip(k):
            banks = psum_bank([P, CHUNK], F32, "spread_psum")
            for i in range(4):
                nc.tensor.transpose(
                    banks[:, i * P : (i + 1) * P], reciprocals[k % 2][:, i : i + 1].to_broadcast([P, P]), ident_f32[:]
                )
            spread[k] = work.tile([P, CHUNK], F32, name="spread", bufs=IN_FLIGHT)
            nc.scalar.copy(out=spread[k][:], in_=banks[:])

        def spread_rows(k):
            spread[k] = work.tile([P, CHUNK], F32, name="spread", bufs=IN_FLIGHT)
            nc.scalar.copy(out=spread[k][:], in_=rows_psum[0][:])

        def quantise_e(k):
            e_words[k] = work.tile([P, CHUNK], U32, name="e_words", bufs=IN_FLIGHT, align_bytes=64)
            e_scales[k] = work.tile([P, CHUNK], U8, name="e_scales", bufs=IN_FLIGHT, align_bytes=64)
            nc.vector.quantize_mx(
                out=e_words[k][:].bitcast(FP8X4), scales=e_scales[k][:], in_=e_grouped[k][:].rearrange("p n t -> p (n t)")
            )

        def make_product(k, j):
            b = k // 4
            summed[k, j] = psum_bank([P, CHUNK], F32, "summed")
            nc.tensor.matmul_mx(
                out=summed[k, j][:],
                lhsT=c3p_words[b][:, j * P : (j + 1) * P].bitcast(FP8X4),
                lhsT_scale=c3p_scales[b][:, j * P : (j + 1) * P],
                rhs=e_words[k][:].bitcast(FP8X4),
                rhs_scale=e_scales[k][:],
                start=True,
                stop=True,
            )

        def use_product(k, j):
            if j == 0:
                result[k] = work.tile([P, PACK, CHUNK], F32, name="result", bufs=IN_FLIGHT)
            nc.vector.scalar_tensor_tensor(
                out=result[k][:, j, :],
                in0=summed[k, j][:],
                scalar=gamma_f32[:, 0:1],
                in1=spread[k][:],
                op0=ALU.mult,
                op1=ALU.mult,
            )
            if j not in vector_adds(k):
                add_x(k, j, nc.gpsimd)

        def vector_adds(k):
            return () if k < 13 else (1, 2, 3) if k == 15 else (2, 3)

        def add_x(k, j, engine):
            engine.tensor_tensor(
                out=result[k][:, j, :],
                in0=result[k][:, j, :],
                in1=x_sb[k // 2][:, j, (k % 2) * CHUNK : (k % 2 + 1) * CHUNK],
                op=ALU.add,
            )

        def store(k, j=None):
            b = k // 4
            pixels = slice((k % 4) * CHUNK, (k % 4 + 1) * CHUNK)
            if j is None:
                nc.sync.dma_start(out=out_view[b][:, :, pixels], in_=result[k][:])
            else:
                nc.sync.dma_start(out=out_view[b][:, j, pixels], in_=result[k][:, j, :])

        def score(c, i):
            make_scores(4 * c + i)
            use_scores(4 * c + i)

        def pooled(part, member):
            make_c3(part, member)
            use_c3(part, member)

        def products(k, tail=False):
            for j in range(4):
                make_product(k, j)
                use_product(k, j)

        def transposes(k):
            transpose_pair(k, 0)
            transpose_pair(k, 1)
            transpose_rows(k)
            copy_pair(k, 0)
            copy_pair(k, 1)
            spread_rows(k)

        def tail_adds(k):
            for j in vector_adds(k):
                add_x(k, j, nc.vector)

        pair_c1(0, "v")
        score(0, 0)
        transpose_w3()
        score(0, 1)
        copy_w3(0, "s")
        copy_w3(1, "s")
        regroup_piece(0, 0, "v")
        regroup_piece(0, 1, "v")
        score(0, 2)
        regroup_piece(1, 0, "s")
        quantise_w3()
        quantise_x(0)
        pooled(0, 0)
        score(0, 3)
        regroup_piece(1, 1, "s")
        regroup_piece(2, 0, "g")
        regroup_piece(2, 1, "g")
        score(1, 0)
        pooled(0, 1)
        score(1, 1)
        pooled(0, 2)
        quantise_x(1)
        pooled(1, 0)
        pooled(0, 3)
        regroup_piece(3, 0, "s")
        regroup_piece(3, 1, "s")
        pooled(1, 1)
        pooled(0, 4)
        pooled(1, 2)
        quantise_x(2)
        pooled(2, 0)
        pooled(1, 3)
        score(1, 2)
        pooled(2, 1)
        pooled(1, 4)
        regroup_piece(4, 0, "g")
        regroup_piece(4, 1, "s")
        pooled(2, 2)
        quantise_x(3)
        pooled(3, 0)
        pooled(2, 3)
        score(1, 3)
        pooled(3, 1)
        pooled(2, 4)
        reciprocal_of_sums(0)
        pooled(3, 2)
        regroup_piece(5, 0, "g")
        regroup_piece(5, 1, "g")
        quantise_x(4)
        transposes(0)
        pooled(3, 3)
        pooled(4, 0)
        score(2, 0)
        pooled(3, 4)
        group_c3p(0, range(4), "g")
        nc.vector.tensor_copy(out=gamma_f32[:], in_=gamma_bf[:])
        for c in range(2, 14):
            part = c + 2
            done = c // 4 if c % 4 == 2 and c > 2 else None
            if c > 2:
                pooled(part, 0)
                score(c, 0)
            if done is not None:
                group_c3p(done, range(0, 2), "s")
            score(c, 1)
            if done is not None:
                group_c3p(done, range(2, 4), "s")
            reciprocal_of_sums(c - 1)
            pooled(part, 1)
            if part + 2 < 16:
                regroup_piece(part + 2, 0, "s")
            score(c, 2)
            pooled(part, 2)
            score(c, 3)
            pooled(part, 3)
            if c >= 3:
                store(c - 3)
            if c % 4 == 2 and c < 13:
                pair_c1((c + 2) // 4, "s")
            if c % 4 == 2:
                quantise_c3p(c // 4)
            quantise_e(c - 2)
            transposes(c - 1)
            if part + 1 < 16:
                quantise_x(part + 1)
            if part + 2 < 16:
                regroup_piece(part + 2, 1, "s")
            pooled(part, 4)
            products(c - 2)

        group_c3p(3, range(4), "s")
        reciprocal_of_sums(13)
        for i in range(4):
            score(14, i)
        transposes(13)
        store(11)
        quantise_e(12)
        quantise_c3p(3)
        score(15, 0)
        score(15, 1)
        reciprocal_of_sums(14)
        products(12)
        transposes(14)
        score(15, 2)
        score(15, 3)
        quantise_e(13)
        tail_adds(12)
        store(12)
        reciprocal_of_sums(15)
        products(13)
        transposes(15)
        quantise_e(14)
        tail_adds(13)
        store(13)
        products(14)
        quantise_e(15)
        tail_adds(14)
        store(14)
        products(15)
        tail_adds(15)
        for j in range(4):
            store(15, j)
